import numpy as np
import ml_dtypes


def mxq(x, axis, fmt="e4m3"):
    dtype, down = {"e4m3": (ml_dtypes.float8_e4m3fn, 7), "e5m2": (ml_dtypes.float8_e5m2, 14)}[fmt]
    v = np.moveaxis(np.asarray(x, np.float32).astype(ml_dtypes.bfloat16).astype(np.float64), axis, -1)
    blocks = v.reshape(v.shape[:-1] + (-1, 32))
    amax = np.abs(blocks).max(-1, keepdims=True)
    byte = np.maximum(np.where(amax > 0, np.frexp(amax)[1] - 1 + 127, 0) - down, 1)
    scale = np.exp2(byte - 127.0)
    codes = (blocks / scale).astype(np.float32).astype(dtype).astype(np.float64)
    return np.moveaxis((codes * scale).reshape(v.shape), -1, axis)


WIDE = False


def mx_kscale(k):
    if not WIDE:
        return np.ones(k)
    levels = np.array([10, -10, 5, -5, 0])
    a = np.random.permutation(np.resize(levels, k // 512 * 4)).reshape(k // 512, 4)
    idx = np.arange(k)
    return np.exp2(a[idx // 512, idx % 128 // 32])


BF16 = ml_dtypes.bfloat16


def bf(x):
    return np.asarray(x, np.float32).astype(BF16)


def f64(x):
    return np.asarray(x).astype(np.float64)


B, N, D, K = 2, 16384, 512, 128

BN_EPS = 1e-5
NORM_EPS = 1e-12


def _l2_normalize(v, axis):
    n = np.sqrt(np.sum(v * v, axis=axis, keepdims=True))
    return v / np.maximum(n, NORM_EPS)


def setup_inputs():
    s = mx_kscale(D)
    mu = np.random.standard_normal(D) * 0.125
    h = np.random.standard_normal(K)
    return {"x": bf((np.random.standard_normal((B, N, D)) + mu) * s),
            "clusters": bf((np.random.standard_normal((D, K)) * 0.5 / np.sqrt(D) + mu[:, None] * h * 0.25 / np.sum(mu * mu)) / s[:, None]),
            "clusters2": bf((mu[:, None] + np.random.standard_normal((1, D, K)) / np.sqrt(D)) * s[:, None]),
            "bn_gamma": bf(1.0 + 0.1 * np.random.standard_normal(K)),
            "bn_beta": bf(0.5 * np.random.standard_normal(K))}


def reference(x, clusters, clusters2, bn_gamma, bn_beta):
    x, clusters, clusters2 = f64(x), f64(clusters), f64(clusters2)
    bn_gamma, bn_beta = f64(bn_gamma), f64(bn_beta)
    B, N, D = x.shape
    K = clusters2.shape[-1]
    x_flat = x.reshape(-1, D)
    assignment = mxq(x_flat, 1, "e4m3") @ mxq(clusters, 0, "e4m3")
    mean = np.mean(assignment, axis=0)
    var = np.var(assignment, axis=0)
    assignment = (assignment - mean) * (1.0 / np.sqrt(var + BN_EPS)) * bn_gamma + bn_beta
    e = np.exp(assignment - assignment.max(axis=1, keepdims=True))
    assignment = (e / e.sum(axis=1, keepdims=True))[:, :K]
    assignment = assignment.reshape(B, N, K)
    a_sum = np.sum(assignment, axis=1, keepdims=True)
    a = a_sum * clusters2
    vlad = (mxq(x, 1, "e4m3").transpose(0, 2, 1) @ mxq(assignment, 1, "e4m3")) - a
    vlad = _l2_normalize(vlad, axis=1)
    vlad = vlad.reshape(B, D * K)
    vlad = _l2_normalize(vlad, axis=1)
    return vlad

@@ -1,0 +1,350 @@
+from contextlib import ExitStack
+
+import concourse.mybir as mybir
+from concourse.masks import make_identity
+
+F32 = mybir.dt.float32
+BF16 = mybir.dt.bfloat16
+U32 = mybir.dt.uint32
+U8 = mybir.dt.uint8
+FP8X4 = mybir.dt.float8_e4m3fn_x4
+ACT = mybir.ActivationFunctionType
+ALU = mybir.AluOpType
+AX = mybir.AxisListType
+
+B, N, D, K = 2, 16384, 512, 128
+P = 128
+PACK = 4
+ROWS = P * PACK
+GROUPS = B * N // ROWS
+GROUPS_PER_BATCH = N // ROWS
+ROUNDS = GROUPS // 2
+BN_EPS = 1e-5
+NORM_EPS = 1e-12
+SCALAR_COLS = 256
+
+FLOPS = 2 * 2 * B * N * D * K
+
+
+def tile_modelnew_k_kernel(tc, x, clusters, clusters2, bn_gamma, bn_beta, out):
+    nc = tc.nc
+    x_groups = x.rearrange("b (g p j) d -> (b g) p (j d)", p=P, j=PACK)
+
+    with ExitStack() as whole:
+        whole.enter_context(tc.manual_schedule())
+        keep = whole.enter_context(tc.tile_pool(name="keep", bufs=1))
+        x_pool = whole.enter_context(tc.tile_pool(name="x_pool", bufs=5))
+        grouped_pool = whole.enter_context(tc.tile_pool(name="grouped_pool", bufs=4))
+
+        ident = keep.tile([P, P], F32)
+        make_identity(nc, ident[:])
+        ones = keep.tile([P, P], F32)
+        nc.vector.memset(ones[:], 1.0)
+        minus_half = keep.tile([P, B], F32)
+        nc.vector.memset(minus_half[:], -0.5)
+        zero = keep.tile([P, 1], F32)
+        nc.vector.memset(zero[:], 0.0)
+        one = keep.tile([P, 1], F32)
+        nc.scalar.activation(out=one[:], in_=zero[:], func=ACT.Exp)
+
+        cl_codes = keep.tile([P, K], U32, align_bytes=64)
+        cl_scales = keep.tile([P, K], U8, align_bytes=64)
+        xd_codes = keep.tile([P, GROUPS, ROWS], U32, align_bytes=64)
+        xd_scales = keep.tile([P, GROUPS, ROWS], U8, align_bytes=64)
+        c2T = keep.tile([P, D], F32)
+        gamma_beta = keep.tile([P, 2], F32)
+        stats = keep.tile([P, GROUPS, 6], F32)
+
+        def load_group(g):
+            x_sb = x_pool.tile([P, PACK * D], BF16)
+            nc.sync.dma_start(out=x_sb[:], in_=x_groups[g])
+            return x_sb
+
+        def cluster_scores(psum_pool, g):
+            aT = psum_pool.tile([P, ROWS], F32)
+            nc.tensor.matmul_mx(
+                out=aT[:],
+                lhsT=cl_codes[:].bitcast(FP8X4),
+                lhsT_scale=cl_scales[:],
+                rhs=xd_codes[:, g, :].bitcast(FP8X4),
+                rhs_scale=xd_scales[:, g, :],
+                start=True,
+                stop=True,
+            )
+            return aT
+
+        with ExitStack() as pass1:
+            setup = pass1.enter_context(tc.tile_pool(name="setup", bufs=1))
+            setup_ps = pass1.enter_context(tc.psum_pool(name="setup_ps", bufs=1))
+            xT_ps = pass1.enter_context(tc.psum_pool(name="xT_ps", bufs=4))
+            aT_ps1 = pass1.enter_context(tc.psum_pool(name="aT_ps1", bufs=2))
+
+            c2_rows = setup.tile([P, PACK, K], BF16)
+            nc.scalar.dma_start(out=c2_rows[:], in_=clusters2.rearrange("o (t p) k -> p (o t) k", p=P))
+            gb_rows = setup.tile([P, P], BF16)
+            nc.vector.memset(gb_rows[:], 0.0)
+            nc.scalar.dma_start(out=gb_rows[0:1, :], in_=bn_gamma.rearrange("(o k) -> o k", o=1))
+            nc.scalar.dma_start(out=gb_rows[1:2, :], in_=bn_beta.rearrange("(o k) -> o k", o=1))
+
+            cl_rows = setup.tile([P, PACK, K], BF16)
+            for u in range(2):
+                nc.sync.dma_start(
+                    out=cl_rows[:, 2 * u : 2 * u + 2, :],
+                    in_=clusters[256 * u : 256 * (u + 1), :].rearrange("(q e) k -> q e k", e=2),
+                )
+            cl_grouped = setup.tile([P, K, PACK], BF16, align_bytes=64)
+            nc.vector.tensor_copy(out=cl_grouped[:], in_=cl_rows[:].rearrange("q t k -> q k t"))
+            nc.vector.quantize_mx(
+                out=cl_codes[:].bitcast(FP8X4),
+                scales=cl_scales[:],
+                in_=cl_grouped[:].rearrange("q k t -> q (k t)"),
+            )
+
+            def transpose_small_inputs():
+                c2_f32 = setup.tile([P, PACK, K], F32)
+                nc.vector.tensor_copy(out=c2_f32[:], in_=c2_rows[:])
+                c2_ps = setup_ps.tile([P, PACK, P], F32)
+                for t in range(PACK):
+                    nc.tensor.transpose(out=c2_ps[:, t, :], in_=c2_f32[:, t, :], identity=ident[:])
+                nc.vector.tensor_copy(out=c2T[:], in_=c2_ps[:].rearrange("k t p -> k (t p)"))
+                gb_f32 = setup.tile([P, P], F32)
+                nc.vector.tensor_copy(out=gb_f32[:], in_=gb_rows[:])
+                gb_ps = setup_ps.tile([P, P], F32)
+                nc.tensor.transpose(out=gb_ps[:], in_=gb_f32[:], identity=ident[:])
+                nc.vector.tensor_copy(out=gamma_beta[:], in_=gb_ps[:, 0:2])
+
+            def transpose_group(g):
+                x_sb = load_group(g)
+                x_words = x_sb[:].bitcast(F32)
+                grouped = grouped_pool.tile([P, PACK * ROWS], BF16, align_bytes=64)
+                grouped_words = grouped[:].bitcast(F32).rearrange("q (c u) -> q c u", u=2)
+                for half in range(2):
+                    xT = xT_ps.tile([P, 2, 2 * P], F32)
+                    for jj in range(2):
+                        j = 2 * half + jj
+                        for u in range(2):
+                            first = 256 * j + 128 * u
+                            nc.tensor.transpose(
+                                out=xT[:, u, P * jj : P * (jj + 1)],
+                                in_=x_words[:, first : first + P],
+                                identity=ident[:],
+                            )
+                    nc.scalar.copy(
+                        out=grouped_words[:, 2 * P * half : 2 * P * (half + 1), :],
+                        in_=xT[:].rearrange("q u c -> q c u"),
+                    )
+                return grouped
+
+            for r in range(ROUNDS + 1):
+                this_round = [2 * r, 2 * r + 1] if r < ROUNDS else []
+                last_round = [2 * r - 2, 2 * r - 1] if r > 0 else []
+                grouped_of = {}
+                for g in this_round:
+                    grouped_of[g] = transpose_group(g)
+                for g in last_round:
+                    aT = cluster_scores(aT_ps1, g)
+                    nc.vector.bn_stats(out=stats[:, g, :], in_=aT[:])
+                for g in this_round:
+                    nc.vector.quantize_mx(
+                        out=xd_codes[:, g, :].bitcast(FP8X4),
+                        scales=xd_scales[:, g, :],
+                        in_=grouped_of[g][:],
+                    )
+                if r == 0:
+                    transpose_small_inputs()
+
+        mean_var = keep.tile([P, 2], F32)
+        nc.vector.bn_aggr(out=mean_var[:], in_=stats[:].rearrange("k g s -> k (g s)"))
+        var_eps = keep.tile([P, 1], F32)
+        nc.vector.tensor_scalar(out=var_eps[:], in0=mean_var[:, 1:2], scalar1=BN_EPS, scalar2=None, op0=ALU.add)
+        inv_std = keep.tile([P, 1], F32)
+        nc.gpsimd.tensor_tensor(out=inv_std[:], in0=var_eps[:], in1=minus_half[:, 0:1], op=ALU.pow)
+        bn_scale = keep.tile([P, 1], F32)
+        nc.vector.tensor_tensor(out=bn_scale[:], in0=inv_std[:], in1=gamma_beta[:, 0:1], op=ALU.mult)
+        mean_scaled = keep.tile([P, 1], F32)
+        nc.vector.tensor_tensor(out=mean_scaled[:], in0=mean_var[:, 0:1], in1=bn_scale[:], op=ALU.mult)
+        bn_shift = keep.tile([P, 1], F32)
+        nc.vector.tensor_tensor(out=bn_shift[:], in0=gamma_beta[:, 1:2], in1=mean_scaled[:], op=ALU.subtract)
+
+        with ExitStack() as pass2:
+            acc_ps = pass2.enter_context(tc.psum_pool(name="acc_ps", bufs=1))
+            aT_ps2 = pass2.enter_context(tc.psum_pool(name="aT_ps2", bufs=2))
+            z_ps = pass2.enter_context(tc.psum_pool(name="z_ps", bufs=2))
+            vladT = [acc_ps.tile([P, D], F32, name="vladT%d" % b) for b in range(B)]
+            p_sum = acc_ps.tile([P, B], F32)
+
+            x_of, grouped_of, xn_of, zT_of, z_of, e_of, p_grouped_of, p_codes_of = {}, {}, {}, {}, {}, {}, {}, {}
+            split = D - SCALAR_COLS
+
+            def regroup(copy, g, first, last):
+                x_rows = x_of[g][:].rearrange("p (j d) -> p j d", j=PACK)
+                grouped_cols = grouped_of[g][:].rearrange("p (d j) -> p d j", j=PACK)
+                copy(
+                    out=grouped_cols[:, first:last, :].rearrange("p (c i) j -> p c j i", i=4),
+                    in_=x_rows[:, :, first:last].rearrange("p j (c i) -> p c j i", i=4),
+                )
+
+            def regroup_on_scalar(g):
+                x_of[g] = load_group(g)
+                grouped_of[g] = grouped_pool.tile([P, PACK * ROWS], BF16, align_bytes=64, name="grouped")
+                regroup(nc.scalar.copy, g, split, D)
+
+            def regroup_on_vector(g):
+                regroup(nc.vector.tensor_copy, g, 0, split)
+
+            def quantise_rows(work, g):
+                xn_codes = work.tile([P, D], U32, align_bytes=64)
+                xn_scales = work.tile([P, D], U8, align_bytes=64)
+                nc.vector.quantize_mx(out=xn_codes[:].bitcast(FP8X4), scales=xn_scales[:], in_=grouped_of[g][:])
+                xn_of[g] = (xn_codes, xn_scales)
+
+            def normalised_scores(work, g):
+                aT = cluster_scores(aT_ps2, g)
+                zT = work.tile([P, ROWS], F32)
+                nc.scalar.activation(out=zT[:], in_=aT[:], func=ACT.Identity, bias=bn_shift[:], scale=bn_scale[:])
+                zT_of[g] = zT
+
+            def transpose_scores(g):
+                z = z_ps.tile([P, PACK, K], F32)
+                for j in range(PACK):
+                    nc.tensor.transpose(out=z[:, j, :], in_=zT_of[g][:, P * j : P * (j + 1)], identity=ident[:])
+                z_of[g] = z
+
+            def exponentials(work, g):
+                z = z_of[g]
+                neg_max = work.tile([P, PACK], F32)
+                nc.vector.tensor_reduce(out=neg_max[:], in_=z[:], axis=AX.X, op=ALU.max, negate=True)
+                e = work.tile([P, PACK, K], F32)
+                e_sum = work.tile([P, PACK], F32)
+                for j in range(PACK):
+                    nc.scalar.activation(
+                        out=e[:, j, :],
+                        in_=z[:, j, :],
+                        func=ACT.Exp,
+                        bias=neg_max[:, j : j + 1],
+                        scale=1.0,
+                        accum_out=e_sum[:, j : j + 1],
+                    )
+                e_of[g] = (e, e_sum)
+
+            def probabilities(work, g):
+                e, e_sum = e_of[g]
+                inv_sum = work.tile([P, PACK], F32)
+                nc.vector.reciprocal(out=inv_sum[:], in_=e_sum[:])
+                p_grouped = work.tile([P, K, PACK], BF16, align_bytes=64)
+                nc.vector.tensor_tensor(
+                    out=p_grouped[:],
+                    in0=e[:].rearrange("p j k -> p k j"),
+                    in1=inv_sum[:].unsqueeze(1).to_broadcast([P, K, PACK]),
+                    op=ALU.mult,
+                )
+                b = g // GROUPS_PER_BATCH
+                for j in range(PACK):
+                    nc.tensor.matmul(
+                        out=p_sum[:, b : b + 1],
+                        lhsT=e[:, j, :],
+                        rhs=inv_sum[:, j : j + 1],
+                        start=g % GROUPS_PER_BATCH == 0 and j == 0,
+                        stop=g % GROUPS_PER_BATCH == GROUPS_PER_BATCH - 1 and j == PACK - 1,
+                    )
+                p_grouped_of[g] = p_grouped
+
+            def quantise_probabilities(work, g):
+                p_codes = work.tile([P, K], U32, align_bytes=64)
+                p_scales = work.tile([P, K], U8, align_bytes=64)
+                nc.vector.quantize_mx(
+                    out=p_codes[:].bitcast(FP8X4),
+                    scales=p_scales[:],
+                    in_=p_grouped_of[g][:].rearrange("p k j -> p (k j)"),
+                )
+                p_codes_of[g] = (p_codes, p_scales)
+
+            def add_to_vlad(g):
+                p_codes, p_scales = p_codes_of[g]
+                xn_codes, xn_scales = xn_of[g]
+                nc.tensor.matmul_mx(
+                    out=vladT[g // GROUPS_PER_BATCH][:],
+                    lhsT=p_codes[:].bitcast(FP8X4),
+                    lhsT_scale=p_scales[:],
+                    rhs=xn_codes[:].bitcast(FP8X4),
+                    rhs_scale=xn_scales[:],
+                    start=g % GROUPS_PER_BATCH == 0,
+                    stop=g % GROUPS_PER_BATCH == GROUPS_PER_BATCH - 1,
+                )
+
+            def exists(g):
+                return 0 <= g < GROUPS
+
+            with tc.tile_pool(name="work", bufs=3) as work:
+                for i in range(-2, GROUPS):
+                    if exists(i + 2):
+                        regroup_on_scalar(i + 2)
+                    if exists(i + 1):
+                        transpose_scores(i + 1)
+                    if exists(i):
+                        probabilities(work, i)
+                    if exists(i + 1):
+                        exponentials(work, i + 1)
+                    if exists(i):
+                        quantise_probabilities(work, i)
+                    if exists(i + 1):
+                        quantise_rows(work, i + 1)
+                    if exists(i + 2):
+                        normalised_scores(work, i + 2)
+                    if exists(i):
+                        add_to_vlad(i)
+                    if exists(i + 2):
+                        regroup_on_vector(i + 2)
+
+            with tc.tile_pool(name="tail", bufs=1) as tail:
+                neg_p_sum = tail.tile([P, B], F32)
+                nc.vector.tensor_scalar(out=neg_p_sum[:], in0=p_sum[:], scalar1=-1.0, scalar2=None, op0=ALU.mult)
+                v = tail.tile([P, B, D], F32)
+                squares = tail.tile([P, B, D], F32)
+                sum_sq = tail.tile([P, B], F32)
+                for b in range(B):
+                    nc.vector.scalar_tensor_tensor(
+                        out=v[:, b, :],
+                        in0=c2T[:],
+                        scalar=neg_p_sum[:, b : b + 1],
+                        in1=vladT[b][:],
+                        op0=ALU.mult,
+                        op1=ALU.add,
+                    )
+                    nc.scalar.activation(
+                        out=squares[:, b, :], in_=v[:, b, :], func=ACT.Square, accum_out=sum_sq[:, b : b + 1]
+                    )
+                floor1 = tail.tile([P, B], F32)
+                nc.vector.tensor_scalar(
+                    out=floor1[:], in0=sum_sq[:], scalar1=NORM_EPS * NORM_EPS, scalar2=None, op0=ALU.max
+                )
+                inv1 = tail.tile([P, B], F32)
+                nc.gpsimd.tensor_tensor(out=inv1[:], in0=floor1[:], in1=minus_half[:], op=ALU.pow)
+                once = tail.tile([P, B], F32)
+                nc.vector.tensor_tensor(out=once[:], in0=sum_sq[:], in1=inv1[:], op=ALU.mult)
+                col_sq = tail.tile([P, B], F32)
+                nc.vector.tensor_tensor(out=col_sq[:], in0=once[:], in1=inv1[:], op=ALU.mult)
+                total_ps = aT_ps2.tile([P, B], F32, tag="aT")
+                nc.tensor.matmul(out=total_ps[:], lhsT=ones[:], rhs=col_sq[:], start=True, stop=True)
+                floor2 = tail.tile([P, B], F32)
+                nc.vector.tensor_scalar(
+                    out=floor2[:], in0=total_ps[:], scalar1=NORM_EPS * NORM_EPS, scalar2=None, op0=ALU.max
+                )
+                inv2 = tail.tile([P, B], F32)
+                nc.gpsimd.tensor_tensor(out=inv2[:], in0=floor2[:], in1=minus_half[:], op=ALU.pow)
+                factor = tail.tile([P, B], F32)
+                nc.vector.tensor_tensor(out=factor[:], in0=inv1[:], in1=inv2[:], op=ALU.mult)
+
+                v_unit = tail.tile([P, B, D], F32)
+                v_out = tail.tile([P, B, PACK, K], F32)
+                for b in range(B):
+                    nc.vector.tensor_scalar(
+                        out=v_unit[:, b, :], in0=v[:, b, :], scalar1=factor[:, b : b + 1], scalar2=None, op0=ALU.mult
+                    )
+                    v_ps = z_ps.tile([P, PACK, K], F32, tag="z")
+                    for t in range(PACK):
+                        nc.tensor.transpose(
+                            out=v_ps[:, t, :], in_=v_unit[:, b, P * t : P * (t + 1)], identity=ident[:]
+                        )
+                    nc.scalar.copy(out=v_out[:, b, :, :], in_=v_ps[:])
+                    nc.sync.dma_start(out=out[b].rearrange("(t p k) -> p t k", p=P, k=K), in_=v_out[:, b, :, :])

@@ -169,11 +169,12 @@ def tile_modelnew_k_kernel(tc, x, clusters, clusters2, bn_gamma, bn_beta, out):
         with ExitStack() as pass2:
             acc_ps = pass2.enter_context(tc.psum_pool(name="acc_ps", bufs=1))
             aT_ps2 = pass2.enter_context(tc.psum_pool(name="aT_ps2", bufs=2))
-            z_ps = pass2.enter_context(tc.psum_pool(name="z_ps", bufs=2))
+            z_ps = pass2.enter_context(tc.psum_pool(name="z_ps", bufs=3))
             vladT = [acc_ps.tile([P, D], F32, name="vladT%d" % b) for b in range(B)]
             p_sum = acc_ps.tile([P, B], F32)
 
-            x_of, grouped_of, xn_of, zT_of, z_of, e_of, p_grouped_of, p_codes_of = {}, {}, {}, {}, {}, {}, {}, {}
+            x_of, grouped_of, xn_of, zT_of, z_of, e_of = {}, {}, {}, {}, {}, {}
+            aT_of, inv_sum_of, p_grouped_of, p_codes_of = {}, {}, {}, {}
             split = D - SCALAR_COLS
 
             def regroup(copy, g, first, last):
@@ -198,10 +199,14 @@ def tile_modelnew_k_kernel(tc, x, clusters, clusters2, bn_gamma, bn_beta, out):
                 nc.vector.quantize_mx(out=xn_codes[:].bitcast(FP8X4), scales=xn_scales[:], in_=grouped_of[g][:])
                 xn_of[g] = (xn_codes, xn_scales)
 
-            def normalised_scores(work, g):
-                aT = cluster_scores(aT_ps2, g)
+            def scores(g):
+                aT_of[g] = cluster_scores(aT_ps2, g)
+
+            def normalise_scores(work, g):
                 zT = work.tile([P, ROWS], F32)
-                nc.scalar.activation(out=zT[:], in_=aT[:], func=ACT.Identity, bias=bn_shift[:], scale=bn_scale[:])
+                nc.scalar.activation(
+                    out=zT[:], in_=aT_of[g][:], func=ACT.Identity, bias=bn_shift[:], scale=bn_scale[:]
+                )
                 zT_of[g] = zT
 
             def transpose_scores(g):
@@ -227,17 +232,11 @@ def tile_modelnew_k_kernel(tc, x, clusters, clusters2, bn_gamma, bn_beta, out):
                     )
                 e_of[g] = (e, e_sum)
 
-            def probabilities(work, g):
+            def inverse_sums(work, g):
                 e, e_sum = e_of[g]
                 inv_sum = work.tile([P, PACK], F32)
                 nc.vector.reciprocal(out=inv_sum[:], in_=e_sum[:])
-                p_grouped = work.tile([P, K, PACK], BF16, align_bytes=64)
-                nc.vector.tensor_tensor(
-                    out=p_grouped[:],
-                    in0=e[:].rearrange("p j k -> p k j"),
-                    in1=inv_sum[:].unsqueeze(1).to_broadcast([P, K, PACK]),
-                    op=ALU.mult,
-                )
+                inv_sum_of[g] = inv_sum
                 b = g // GROUPS_PER_BATCH
                 for j in range(PACK):
                     nc.tensor.matmul(
@@ -247,6 +246,16 @@ def tile_modelnew_k_kernel(tc, x, clusters, clusters2, bn_gamma, bn_beta, out):
                         start=g % GROUPS_PER_BATCH == 0 and j == 0,
                         stop=g % GROUPS_PER_BATCH == GROUPS_PER_BATCH - 1 and j == PACK - 1,
                     )
+
+            def probabilities(work, g):
+                e, e_sum = e_of[g]
+                p_grouped = work.tile([P, K, PACK], BF16, align_bytes=64)
+                nc.vector.tensor_tensor(
+                    out=p_grouped[:],
+                    in0=e[:].rearrange("p j k -> p k j"),
+                    in1=inv_sum_of[g][:].unsqueeze(1).to_broadcast([P, K, PACK]),
+                    op=ALU.mult,
+                )
                 p_grouped_of[g] = p_grouped
 
             def quantise_probabilities(work, g):
@@ -276,25 +285,29 @@ def tile_modelnew_k_kernel(tc, x, clusters, clusters2, bn_gamma, bn_beta, out):
                 return 0 <= g < GROUPS
 
             with tc.tile_pool(name="work", bufs=3) as work:
-                for i in range(-2, GROUPS):
+                for i in range(-3, GROUPS + 1):
                     if exists(i + 2):
                         regroup_on_scalar(i + 2)
-                    if exists(i + 1):
-                        transpose_scores(i + 1)
-                    if exists(i):
-                        probabilities(work, i)
+                    if exists(i - 1):
+                        add_to_vlad(i - 1)
+                    if exists(i + 3):
+                        scores(i + 3)
+                    if exists(i + 2):
+                        transpose_scores(i + 2)
                     if exists(i + 1):
                         exponentials(work, i + 1)
                     if exists(i):
-                        quantise_probabilities(work, i)
+                        inverse_sums(work, i)
                     if exists(i + 1):
                         quantise_rows(work, i + 1)
-                    if exists(i + 2):
-                        normalised_scores(work, i + 2)
                     if exists(i):
-                        add_to_vlad(i)
+                        probabilities(work, i)
+                    if exists(i + 3):
+                        normalise_scores(work, i + 3)
                     if exists(i + 2):
                         regroup_on_vector(i + 2)
+                    if exists(i):
+                        quantise_probabilities(work, i)
 
             with tc.tile_pool(name="tail", bufs=1) as tail:
                 neg_p_sum = tail.tile([P, B], F32)

@@ -22,6 +22,7 @@ ROUNDS = GROUPS // 2
 BN_EPS = 1e-5
 NORM_EPS = 1e-12
 SCALAR_COLS = 256
+SUM_COLS = 32
 
 FLOPS = 2 * 2 * B * N * D * K
 
@@ -171,7 +172,7 @@ def tile_modelnew_k_kernel(tc, x, clusters, clusters2, bn_gamma, bn_beta, out):
             aT_ps2 = pass2.enter_context(tc.psum_pool(name="aT_ps2", bufs=2))
             z_ps = pass2.enter_context(tc.psum_pool(name="z_ps", bufs=3))
             vladT = [acc_ps.tile([P, D], F32, name="vladT%d" % b) for b in range(B)]
-            p_sum = acc_ps.tile([P, B], F32)
+            p_sum = acc_ps.tile([P, B, SUM_COLS], F32)
 
             x_of, grouped_of, xn_of, zT_of, z_of, e_of = {}, {}, {}, {}, {}, {}
             aT_of, inv_sum_of, p_grouped_of, p_codes_of = {}, {}, {}, {}
@@ -240,9 +241,9 @@ def tile_modelnew_k_kernel(tc, x, clusters, clusters2, bn_gamma, bn_beta, out):
                 b = g // GROUPS_PER_BATCH
                 for j in range(PACK):
                     nc.tensor.matmul(
-                        out=p_sum[:, b : b + 1],
+                        out=p_sum[:, b, :],
                         lhsT=e[:, j, :],
-                        rhs=inv_sum[:, j : j + 1],
+                        rhs=inv_sum[:, j : j + 1].to_broadcast([P, SUM_COLS]),
                         start=g % GROUPS_PER_BATCH == 0 and j == 0,
                         stop=g % GROUPS_PER_BATCH == GROUPS_PER_BATCH - 1 and j == PACK - 1,
                     )
@@ -311,7 +312,7 @@ def tile_modelnew_k_kernel(tc, x, clusters, clusters2, bn_gamma, bn_beta, out):
 
             with tc.tile_pool(name="tail", bufs=1) as tail:
                 neg_p_sum = tail.tile([P, B], F32)
-                nc.vector.tensor_scalar(out=neg_p_sum[:], in0=p_sum[:], scalar1=-1.0, scalar2=None, op0=ALU.mult)
+                nc.vector.tensor_scalar(out=neg_p_sum[:], in0=p_sum[:, :, 0], scalar1=-1.0, scalar2=None, op0=ALU.mult)
                 v = tail.tile([P, B, D], F32)
                 squares = tail.tile([P, B, D], F32)
                 sum_sq = tail.tile([P, B], F32)

@@ -23,6 +23,7 @@ BN_EPS = 1e-5
 NORM_EPS = 1e-12
 SCALAR_COLS = 256
 SUM_COLS = 32
+EARLY = 2
 
 FLOPS = 2 * 2 * B * N * D * K
 
@@ -76,10 +77,15 @@ def tile_modelnew_k_kernel(tc, x, clusters, clusters2, bn_gamma, bn_beta, out):
 
         with ExitStack() as pass1:
             setup = pass1.enter_context(tc.tile_pool(name="setup", bufs=1))
-            setup_ps = pass1.enter_context(tc.psum_pool(name="setup_ps", bufs=1))
-            xT_ps = pass1.enter_context(tc.psum_pool(name="xT_ps", bufs=4))
+            xT_ps = pass1.enter_context(tc.psum_pool(name="xT_ps", bufs=6))
             aT_ps1 = pass1.enter_context(tc.psum_pool(name="aT_ps1", bufs=2))
 
+            cl_rows = setup.tile([P, PACK, K], BF16)
+            for u in range(2):
+                nc.scalar.dma_start(
+                    out=cl_rows[:, 2 * u : 2 * u + 2, :],
+                    in_=clusters[256 * u : 256 * (u + 1), :].rearrange("(q e) k -> q e k", e=2),
+                )
             c2_rows = setup.tile([P, PACK, K], BF16)
             nc.scalar.dma_start(out=c2_rows[:], in_=clusters2.rearrange("o (t p) k -> p (o t) k", p=P))
             gb_rows = setup.tile([P, P], BF16)
@@ -87,12 +93,6 @@ def tile_modelnew_k_kernel(tc, x, clusters, clusters2, bn_gamma, bn_beta, out):
             nc.scalar.dma_start(out=gb_rows[0:1, :], in_=bn_gamma.rearrange("(o k) -> o k", o=1))
             nc.scalar.dma_start(out=gb_rows[1:2, :], in_=bn_beta.rearrange("(o k) -> o k", o=1))
 
-            cl_rows = setup.tile([P, PACK, K], BF16)
-            for u in range(2):
-                nc.sync.dma_start(
-                    out=cl_rows[:, 2 * u : 2 * u + 2, :],
-                    in_=clusters[256 * u : 256 * (u + 1), :].rearrange("(q e) k -> q e k", e=2),
-                )
             cl_grouped = setup.tile([P, K, PACK], BF16, align_bytes=64)
             nc.vector.tensor_copy(out=cl_grouped[:], in_=cl_rows[:].rearrange("q t k -> q k t"))
             nc.vector.quantize_mx(
@@ -100,17 +100,17 @@ def tile_modelnew_k_kernel(tc, x, clusters, clusters2, bn_gamma, bn_beta, out):
                 scales=cl_scales[:],
                 in_=cl_grouped[:].rearrange("q k t -> q (k t)"),
             )
+            c2_f32 = setup.tile([P, PACK, K], F32)
+            nc.vector.tensor_copy(out=c2_f32[:], in_=c2_rows[:])
+            gb_f32 = setup.tile([P, P], F32)
+            nc.vector.tensor_copy(out=gb_f32[:], in_=gb_rows[:])
 
             def transpose_small_inputs():
-                c2_f32 = setup.tile([P, PACK, K], F32)
-                nc.vector.tensor_copy(out=c2_f32[:], in_=c2_rows[:])
-                c2_ps = setup_ps.tile([P, PACK, P], F32)
+                c2_ps = xT_ps.tile([P, PACK, P], F32, tag="xT")
                 for t in range(PACK):
                     nc.tensor.transpose(out=c2_ps[:, t, :], in_=c2_f32[:, t, :], identity=ident[:])
                 nc.vector.tensor_copy(out=c2T[:], in_=c2_ps[:].rearrange("k t p -> k (t p)"))
-                gb_f32 = setup.tile([P, P], F32)
-                nc.vector.tensor_copy(out=gb_f32[:], in_=gb_rows[:])
-                gb_ps = setup_ps.tile([P, P], F32)
+                gb_ps = xT_ps.tile([P, P], F32, tag="xT")
                 nc.tensor.transpose(out=gb_ps[:], in_=gb_f32[:], identity=ident[:])
                 nc.vector.tensor_copy(out=gamma_beta[:], in_=gb_ps[:, 0:2])
 
@@ -154,12 +154,34 @@ def tile_modelnew_k_kernel(tc, x, clusters, clusters2, bn_gamma, bn_beta, out):
                 if r == 0:
                     transpose_small_inputs()
 
+        x_of, grouped_of = {}, {}
+        split = D - SCALAR_COLS
+
+        def regroup(copy, g, first, last):
+            x_rows = x_of[g][:].rearrange("p (j d) -> p j d", j=PACK)
+            grouped_cols = grouped_of[g][:].rearrange("p (d j) -> p d j", j=PACK)
+            copy(
+                out=grouped_cols[:, first:last, :].rearrange("p (c i) j -> p c j i", i=4),
+                in_=x_rows[:, :, first:last].rearrange("p j (c i) -> p c j i", i=4),
+            )
+
+        def regroup_on_scalar(g):
+            x_of[g] = load_group(g)
+            grouped_of[g] = grouped_pool.tile([P, PACK * ROWS], BF16, align_bytes=64, name="grouped")
+            regroup(nc.scalar.copy, g, split, D)
+
+        def regroup_on_vector(g):
+            regroup(nc.vector.tensor_copy, g, 0, split)
+
         mean_var = keep.tile([P, 2], F32)
         nc.vector.bn_aggr(out=mean_var[:], in_=stats[:].rearrange("k g s -> k (g s)"))
         var_eps = keep.tile([P, 1], F32)
         nc.vector.tensor_scalar(out=var_eps[:], in0=mean_var[:, 1:2], scalar1=BN_EPS, scalar2=None, op0=ALU.add)
         inv_std = keep.tile([P, 1], F32)
         nc.gpsimd.tensor_tensor(out=inv_std[:], in0=var_eps[:], in1=minus_half[:, 0:1], op=ALU.pow)
+        for g in range(EARLY):
+            regroup_on_scalar(g)
+            regroup_on_vector(g)
         bn_scale = keep.tile([P, 1], F32)
         nc.vector.tensor_tensor(out=bn_scale[:], in0=inv_std[:], in1=gamma_beta[:, 0:1], op=ALU.mult)
         mean_scaled = keep.tile([P, 1], F32)
@@ -174,25 +196,7 @@ def tile_modelnew_k_kernel(tc, x, clusters, clusters2, bn_gamma, bn_beta, out):
             vladT = [acc_ps.tile([P, D], F32, name="vladT%d" % b) for b in range(B)]
             p_sum = acc_ps.tile([P, B, SUM_COLS], F32)
 
-            x_of, grouped_of, xn_of, zT_of, z_of, e_of = {}, {}, {}, {}, {}, {}
-            aT_of, inv_sum_of, p_grouped_of, p_codes_of = {}, {}, {}, {}
-            split = D - SCALAR_COLS
-
-            def regroup(copy, g, first, last):
-                x_rows = x_of[g][:].rearrange("p (j d) -> p j d", j=PACK)
-                grouped_cols = grouped_of[g][:].rearrange("p (d j) -> p d j", j=PACK)
-                copy(
-                    out=grouped_cols[:, first:last, :].rearrange("p (c i) j -> p c j i", i=4),
-                    in_=x_rows[:, :, first:last].rearrange("p j (c i) -> p c j i", i=4),
-                )
-
-            def regroup_on_scalar(g):
-                x_of[g] = load_group(g)
-                grouped_of[g] = grouped_pool.tile([P, PACK * ROWS], BF16, align_bytes=64, name="grouped")
-                regroup(nc.scalar.copy, g, split, D)
-
-            def regroup_on_vector(g):
-                regroup(nc.vector.tensor_copy, g, 0, split)
+            xn_of, aT_of, zT_of, z_of, e_of, inv_sum_of, p_grouped_of, p_codes_of = {}, {}, {}, {}, {}, {}, {}, {}
 
             def quantise_rows(work, g):
                 xn_codes = work.tile([P, D], U32, align_bytes=64)
@@ -282,12 +286,12 @@ def tile_modelnew_k_kernel(tc, x, clusters, clusters2, bn_gamma, bn_beta, out):
                     stop=g % GROUPS_PER_BATCH == GROUPS_PER_BATCH - 1,
                 )
 
-            def exists(g):
-                return 0 <= g < GROUPS
+            def exists(g, first=0):
+                return first <= g < GROUPS
 
             with tc.tile_pool(name="work", bufs=3) as work:
                 for i in range(-3, GROUPS + 1):
-                    if exists(i + 2):
+                    if exists(i + 2, first=EARLY):
                         regroup_on_scalar(i + 2)
                     if exists(i - 1):
                         add_to_vlad(i - 1)
@@ -305,7 +309,7 @@ def tile_modelnew_k_kernel(tc, x, clusters, clusters2, bn_gamma, bn_beta, out):
                         probabilities(work, i)
                     if exists(i + 3):
                         normalise_scores(work, i + 3)
-                    if exists(i + 2):
+                    if exists(i + 2, first=EARLY):
                         regroup_on_vector(i + 2)
                     if exists(i):
                         quantise_probabilities(work, i)

@@ -23,6 +23,7 @@ BN_EPS = 1e-5
 NORM_EPS = 1e-12
 SCALAR_COLS = 256
 SUM_COLS = 32
+SCORE_LAG = 2
 EARLY = 2
 
 FLOPS = 2 * 2 * B * N * D * K
@@ -136,9 +137,10 @@ def tile_modelnew_k_kernel(tc, x, clusters, clusters2, bn_gamma, bn_beta, out):
                     )
                 return grouped
 
-            for r in range(ROUNDS + 1):
+            for r in range(ROUNDS + SCORE_LAG):
                 this_round = [2 * r, 2 * r + 1] if r < ROUNDS else []
-                last_round = [2 * r - 2, 2 * r - 1] if r > 0 else []
+                s = r - SCORE_LAG
+                last_round = [2 * s, 2 * s + 1] if s >= 0 else []
                 grouped_of = {}
                 for g in this_round:
                     grouped_of[g] = transpose_group(g)

@@ -24,7 +24,11 @@ NORM_EPS = 1e-12
 SCALAR_COLS = 256
 SUM_COLS = 32
 SCORE_LAG = 2
-EARLY = 2
+FIRST_PIECES = 2
+C2_ROUND = 2
+EARLY_CODES = 2
+PLANES = 4
+EARLY = 3
 
 FLOPS = 2 * 2 * B * N * D * K
 
@@ -37,7 +41,7 @@ def tile_modelnew_k_kernel(tc, x, clusters, clusters2, bn_gamma, bn_beta, out):
         whole.enter_context(tc.manual_schedule())
         keep = whole.enter_context(tc.tile_pool(name="keep", bufs=1))
         x_pool = whole.enter_context(tc.tile_pool(name="x_pool", bufs=5))
-        grouped_pool = whole.enter_context(tc.tile_pool(name="grouped_pool", bufs=4))
+        grouped_pool = whole.enter_context(tc.tile_pool(name="grouped_pool", bufs=5))
 
         ident = keep.tile([P, P], F32)
         make_identity(nc, ident[:])
@@ -53,15 +57,24 @@ def tile_modelnew_k_kernel(tc, x, clusters, clusters2, bn_gamma, bn_beta, out):
         cl_codes = keep.tile([P, K], U32, align_bytes=64)
         cl_scales = keep.tile([P, K], U8, align_bytes=64)
         xd_codes = keep.tile([P, GROUPS, ROWS], U32, align_bytes=64)
-        xd_scales = keep.tile([P, GROUPS, ROWS], U8, align_bytes=64)
+        xd_scales = keep.tile([P, GROUPS // PLANES, ROWS], U8, align_bytes=64)
+        c2_rows = keep.tile([P, PACK, K], BF16)
+        c2_f32 = keep.tile([P, PACK, K], F32)
         c2T = keep.tile([P, D], F32)
         gamma_beta = keep.tile([P, 2], F32)
         stats = keep.tile([P, GROUPS, 6], F32)
 
-        def load_group(g):
+        def load_group(g, pieces=1):
             x_sb = x_pool.tile([P, PACK * D], BF16)
-            nc.sync.dma_start(out=x_sb[:], in_=x_groups[g])
+            width = PACK * D // pieces
+            for i in range(pieces):
+                cols = slice(i * width, (i + 1) * width)
+                nc.sync.dma_start(out=x_sb[:, cols], in_=x_groups[g][:, cols])
             return x_sb
+
+        def scale_plane(g):
+            first = 4 * (g // (GROUPS // PLANES))
+            return xd_scales[first:P, g % (GROUPS // PLANES), :]
 
         def cluster_scores(psum_pool, g):
             aT = psum_pool.tile([P, ROWS], F32)
@@ -70,7 +83,7 @@ def tile_modelnew_k_kernel(tc, x, clusters, clusters2, bn_gamma, bn_beta, out):
                 lhsT=cl_codes[:].bitcast(FP8X4),
                 lhsT_scale=cl_scales[:],
                 rhs=xd_codes[:, g, :].bitcast(FP8X4),
-                rhs_scale=xd_scales[:, g, :],
+                rhs_scale=scale_plane(g),
                 start=True,
                 stop=True,
             )
@@ -87,8 +100,6 @@ def tile_modelnew_k_kernel(tc, x, clusters, clusters2, bn_gamma, bn_beta, out):
                     out=cl_rows[:, 2 * u : 2 * u + 2, :],
                     in_=clusters[256 * u : 256 * (u + 1), :].rearrange("(q e) k -> q e k", e=2),
                 )
-            c2_rows = setup.tile([P, PACK, K], BF16)
-            nc.scalar.dma_start(out=c2_rows[:], in_=clusters2.rearrange("o (t p) k -> p (o t) k", p=P))
             gb_rows = setup.tile([P, P], BF16)
             nc.vector.memset(gb_rows[:], 0.0)
             nc.scalar.dma_start(out=gb_rows[0:1, :], in_=bn_gamma.rearrange("(o k) -> o k", o=1))
@@ -101,22 +112,16 @@ def tile_modelnew_k_kernel(tc, x, clusters, clusters2, bn_gamma, bn_beta, out):
                 scales=cl_scales[:],
                 in_=cl_grouped[:].rearrange("q k t -> q (k t)"),
             )
-            c2_f32 = setup.tile([P, PACK, K], F32)
-            nc.vector.tensor_copy(out=c2_f32[:], in_=c2_rows[:])
             gb_f32 = setup.tile([P, P], F32)
             nc.vector.tensor_copy(out=gb_f32[:], in_=gb_rows[:])
 
-            def transpose_small_inputs():
-                c2_ps = xT_ps.tile([P, PACK, P], F32, tag="xT")
-                for t in range(PACK):
-                    nc.tensor.transpose(out=c2_ps[:, t, :], in_=c2_f32[:, t, :], identity=ident[:])
-                nc.vector.tensor_copy(out=c2T[:], in_=c2_ps[:].rearrange("k t p -> k (t p)"))
+            def transpose_gamma_beta():
                 gb_ps = xT_ps.tile([P, P], F32, tag="xT")
                 nc.tensor.transpose(out=gb_ps[:], in_=gb_f32[:], identity=ident[:])
                 nc.vector.tensor_copy(out=gamma_beta[:], in_=gb_ps[:, 0:2])
 
             def transpose_group(g):
-                x_sb = load_group(g)
+                x_sb = load_group(g, pieces=FIRST_PIECES if g == 0 else 1)
                 x_words = x_sb[:].bitcast(F32)
                 grouped = grouped_pool.tile([P, PACK * ROWS], BF16, align_bytes=64)
                 grouped_words = grouped[:].bitcast(F32).rearrange("q (c u) -> q c u", u=2)
@@ -150,11 +155,13 @@ def tile_modelnew_k_kernel(tc, x, clusters, clusters2, bn_gamma, bn_beta, out):
                 for g in this_round:
                     nc.vector.quantize_mx(
                         out=xd_codes[:, g, :].bitcast(FP8X4),
-                        scales=xd_scales[:, g, :],
+                        scales=scale_plane(g),
                         in_=grouped_of[g][:],
                     )
                 if r == 0:
-                    transpose_small_inputs()
+                    transpose_gamma_beta()
+                if r == C2_ROUND:
+                    nc.sync.dma_start(out=c2_rows[:], in_=clusters2.rearrange("o (t p) k -> p (o t) k", p=P))
 
         x_of, grouped_of = {}, {}
         split = D - SCALAR_COLS
@@ -167,29 +174,48 @@ def tile_modelnew_k_kernel(tc, x, clusters, clusters2, bn_gamma, bn_beta, out):
                 in_=x_rows[:, :, first:last].rearrange("p j (c i) -> p c j i", i=4),
             )
 
-        def regroup_on_scalar(g):
+        def regroup_on_scalar(g, first=split):
             x_of[g] = load_group(g)
             grouped_of[g] = grouped_pool.tile([P, PACK * ROWS], BF16, align_bytes=64, name="grouped")
-            regroup(nc.scalar.copy, g, split, D)
+            regroup(nc.scalar.copy, g, first, D)
 
         def regroup_on_vector(g):
             regroup(nc.vector.tensor_copy, g, 0, split)
 
+        codes_pool = whole.enter_context(tc.tile_pool(name="codes_pool", bufs=3))
+        xn_of = {}
+
+        def quantise_rows(g):
+            xn_codes = codes_pool.tile([P, D], U32, align_bytes=64)
+            xn_scales = codes_pool.tile([P, D], U8, align_bytes=64)
+            nc.vector.quantize_mx(out=xn_codes[:].bitcast(FP8X4), scales=xn_scales[:], in_=grouped_of[g][:])
+            xn_of[g] = (xn_codes, xn_scales)
+
+        for g in range(EARLY):
+            regroup_on_scalar(g, first=0)
         mean_var = keep.tile([P, 2], F32)
         nc.vector.bn_aggr(out=mean_var[:], in_=stats[:].rearrange("k g s -> k (g s)"))
         var_eps = keep.tile([P, 1], F32)
         nc.vector.tensor_scalar(out=var_eps[:], in0=mean_var[:, 1:2], scalar1=BN_EPS, scalar2=None, op0=ALU.add)
         inv_std = keep.tile([P, 1], F32)
         nc.gpsimd.tensor_tensor(out=inv_std[:], in0=var_eps[:], in1=minus_half[:, 0:1], op=ALU.pow)
-        for g in range(EARLY):
-            regroup_on_scalar(g)
-            regroup_on_vector(g)
+        neg_mean = keep.tile([P, 1], F32)
+        nc.vector.tensor_scalar(out=neg_mean[:], in0=mean_var[:, 0:1], scalar1=-1.0, scalar2=None, op0=ALU.mult)
+        quantise_rows(0)
+        nc.vector.tensor_copy(out=c2_f32[:], in_=c2_rows[:])
         bn_scale = keep.tile([P, 1], F32)
         nc.vector.tensor_tensor(out=bn_scale[:], in0=inv_std[:], in1=gamma_beta[:, 0:1], op=ALU.mult)
-        mean_scaled = keep.tile([P, 1], F32)
-        nc.vector.tensor_tensor(out=mean_scaled[:], in0=mean_var[:, 0:1], in1=bn_scale[:], op=ALU.mult)
         bn_shift = keep.tile([P, 1], F32)
-        nc.vector.tensor_tensor(out=bn_shift[:], in0=gamma_beta[:, 1:2], in1=mean_scaled[:], op=ALU.subtract)
+        nc.vector.scalar_tensor_tensor(
+            out=bn_shift[:],
+            in0=neg_mean[:],
+            scalar=bn_scale[:],
+            in1=gamma_beta[:, 1:2],
+            op0=ALU.mult,
+            op1=ALU.add,
+        )
+        for g in range(1, EARLY_CODES):
+            quantise_rows(g)
 
         with ExitStack() as pass2:
             acc_ps = pass2.enter_context(tc.psum_pool(name="acc_ps", bufs=1))
@@ -198,13 +224,7 @@ def tile_modelnew_k_kernel(tc, x, clusters, clusters2, bn_gamma, bn_beta, out):
             vladT = [acc_ps.tile([P, D], F32, name="vladT%d" % b) for b in range(B)]
             p_sum = acc_ps.tile([P, B, SUM_COLS], F32)
 
-            xn_of, aT_of, zT_of, z_of, e_of, inv_sum_of, p_grouped_of, p_codes_of = {}, {}, {}, {}, {}, {}, {}, {}
-
-            def quantise_rows(work, g):
-                xn_codes = work.tile([P, D], U32, align_bytes=64)
-                xn_scales = work.tile([P, D], U8, align_bytes=64)
-                nc.vector.quantize_mx(out=xn_codes[:].bitcast(FP8X4), scales=xn_scales[:], in_=grouped_of[g][:])
-                xn_of[g] = (xn_codes, xn_scales)
+            aT_of, zT_of, z_of, e_of, inv_sum_of, p_grouped_of, p_codes_of = {}, {}, {}, {}, {}, {}, {}
 
             def scores(g):
                 aT_of[g] = cluster_scores(aT_ps2, g)
@@ -291,12 +311,46 @@ def tile_modelnew_k_kernel(tc, x, clusters, clusters2, bn_gamma, bn_beta, out):
             def exists(g, first=0):
                 return first <= g < GROUPS
 
+            c2_ps = z_ps.tile([P, PACK, P], F32, tag="z")
+            for t in range(PACK):
+                nc.tensor.transpose(out=c2_ps[:, t, :], in_=c2_f32[:, t, :], identity=ident[:])
+            nc.vector.tensor_copy(out=c2T[:], in_=c2_ps[:].rearrange("k t p -> k (t p)"))
+
+            tail = pass2.enter_context(tc.tile_pool(name="tail", bufs=1))
+            neg_p_sum = tail.tile([P, B], F32)
+            v = tail.tile([P, B, D], F32)
+            squares = tail.tile([P, B, D], F32)
+            sum_sq = tail.tile([P, B], F32)
+
+            def negate_p_sum(b):
+                nc.vector.tensor_scalar(
+                    out=neg_p_sum[:, b : b + 1], in0=p_sum[:, b, 0:1], scalar1=-1.0, scalar2=None, op0=ALU.mult
+                )
+
+            def finish_vlad(b):
+                nc.vector.scalar_tensor_tensor(
+                    out=v[:, b, :],
+                    in0=c2T[:],
+                    scalar=neg_p_sum[:, b : b + 1],
+                    in1=vladT[b][:],
+                    op0=ALU.mult,
+                    op1=ALU.add,
+                )
+                nc.scalar.activation(
+                    out=squares[:, b, :], in_=v[:, b, :], func=ACT.Square, accum_out=sum_sq[:, b : b + 1]
+                )
+
             with tc.tile_pool(name="work", bufs=3) as work:
                 for i in range(-3, GROUPS + 1):
                     if exists(i + 2, first=EARLY):
                         regroup_on_scalar(i + 2)
                     if exists(i - 1):
                         add_to_vlad(i - 1)
+                    if i == GROUPS_PER_BATCH + 1:
+                        negate_p_sum(0)
+                    if i == GROUPS:
+                        finish_vlad(0)
+                        negate_p_sum(1)
                     if exists(i + 3):
                         scores(i + 3)
                     if exists(i + 2):
@@ -305,8 +359,8 @@ def tile_modelnew_k_kernel(tc, x, clusters, clusters2, bn_gamma, bn_beta, out):
                         exponentials(work, i + 1)
                     if exists(i):
                         inverse_sums(work, i)
-                    if exists(i + 1):
-                        quantise_rows(work, i + 1)
+                    if exists(i + 1, first=EARLY_CODES):
+                        quantise_rows(i + 1)
                     if exists(i):
                         probabilities(work, i)
                     if exists(i + 3):
@@ -316,55 +370,40 @@ def tile_modelnew_k_kernel(tc, x, clusters, clusters2, bn_gamma, bn_beta, out):
                     if exists(i):
                         quantise_probabilities(work, i)
 
-            with tc.tile_pool(name="tail", bufs=1) as tail:
-                neg_p_sum = tail.tile([P, B], F32)
-                nc.vector.tensor_scalar(out=neg_p_sum[:], in0=p_sum[:, :, 0], scalar1=-1.0, scalar2=None, op0=ALU.mult)
-                v = tail.tile([P, B, D], F32)
-                squares = tail.tile([P, B, D], F32)
-                sum_sq = tail.tile([P, B], F32)
-                for b in range(B):
-                    nc.vector.scalar_tensor_tensor(
-                        out=v[:, b, :],
-                        in0=c2T[:],
-                        scalar=neg_p_sum[:, b : b + 1],
-                        in1=vladT[b][:],
-                        op0=ALU.mult,
-                        op1=ALU.add,
-                    )
-                    nc.scalar.activation(
-                        out=squares[:, b, :], in_=v[:, b, :], func=ACT.Square, accum_out=sum_sq[:, b : b + 1]
-                    )
-                floor1 = tail.tile([P, B], F32)
-                nc.vector.tensor_scalar(
-                    out=floor1[:], in0=sum_sq[:], scalar1=NORM_EPS * NORM_EPS, scalar2=None, op0=ALU.max
-                )
-                inv1 = tail.tile([P, B], F32)
-                nc.gpsimd.tensor_tensor(out=inv1[:], in0=floor1[:], in1=minus_half[:], op=ALU.pow)
-                once = tail.tile([P, B], F32)
-                nc.vector.tensor_tensor(out=once[:], in0=sum_sq[:], in1=inv1[:], op=ALU.mult)
-                col_sq = tail.tile([P, B], F32)
-                nc.vector.tensor_tensor(out=col_sq[:], in0=once[:], in1=inv1[:], op=ALU.mult)
-                total_ps = aT_ps2.tile([P, B], F32, tag="aT")
-                nc.tensor.matmul(out=total_ps[:], lhsT=ones[:], rhs=col_sq[:], start=True, stop=True)
-                floor2 = tail.tile([P, B], F32)
-                nc.vector.tensor_scalar(
-                    out=floor2[:], in0=total_ps[:], scalar1=NORM_EPS * NORM_EPS, scalar2=None, op0=ALU.max
-                )
-                inv2 = tail.tile([P, B], F32)
-                nc.gpsimd.tensor_tensor(out=inv2[:], in0=floor2[:], in1=minus_half[:], op=ALU.pow)
-                factor = tail.tile([P, B], F32)
-                nc.vector.tensor_tensor(out=factor[:], in0=inv1[:], in1=inv2[:], op=ALU.mult)
+            finish_vlad(1)
+            floor1 = tail.tile([P, B], F32)
+            nc.vector.tensor_scalar(
+                out=floor1[:], in0=sum_sq[:], scalar1=NORM_EPS * NORM_EPS, scalar2=None, op0=ALU.max
+            )
+            inv1 = tail.tile([P, B], F32)
+            nc.gpsimd.tensor_tensor(out=inv1[:], in0=floor1[:], in1=minus_half[:], op=ALU.pow)
+            inv_floor1 = tail.tile([P, B], F32)
+            nc.vector.reciprocal(out=inv_floor1[:], in_=floor1[:])
+            col_sq = tail.tile([P, B], F32)
+            nc.vector.tensor_tensor(out=col_sq[:], in0=sum_sq[:], in1=inv_floor1[:], op=ALU.mult)
+            total_ps = aT_ps2.tile([P, B], F32, tag="aT")
+            nc.tensor.matmul(out=total_ps[:], lhsT=ones[:], rhs=col_sq[:], start=True, stop=True)
+            floor2 = tail.tile([P, B], F32)
+            nc.vector.tensor_scalar(
+                out=floor2[:], in0=total_ps[:], scalar1=NORM_EPS * NORM_EPS, scalar2=None, op0=ALU.max
+            )
+            inv2 = tail.tile([P, B], F32)
+            nc.gpsimd.tensor_tensor(out=inv2[:], in0=floor2[:], in1=minus_half[:], op=ALU.pow)
 
-                v_unit = tail.tile([P, B, D], F32)
-                v_out = tail.tile([P, B, PACK, K], F32)
-                for b in range(B):
-                    nc.vector.tensor_scalar(
-                        out=v_unit[:, b, :], in0=v[:, b, :], scalar1=factor[:, b : b + 1], scalar2=None, op0=ALU.mult
-                    )
-                    v_ps = z_ps.tile([P, PACK, K], F32, tag="z")
-                    for t in range(PACK):
-                        nc.tensor.transpose(
-                            out=v_ps[:, t, :], in_=v_unit[:, b, P * t : P * (t + 1)], identity=ident[:]
-                        )
-                    nc.scalar.copy(out=v_out[:, b, :, :], in_=v_ps[:])
-                    nc.sync.dma_start(out=out[b].rearrange("(t p k) -> p t k", p=P, k=K), in_=v_out[:, b, :, :])
+            v_unit = tail.tile([P, B, D], F32)
+            v_out = tail.tile([P, B, PACK, K], F32)
+            v_ps = []
+            for b in range(B):
+                nc.vector.tensor_scalar(
+                    out=v_unit[:, b, :], in0=v[:, b, :], scalar1=inv1[:, b : b + 1], scalar2=None, op0=ALU.mult
+                )
+                v_b = z_ps.tile([P, PACK, K], F32, tag="z")
+                for t in range(PACK):
+                    nc.tensor.transpose(out=v_b[:, t, :], in_=v_unit[:, b, P * t : P * (t + 1)], identity=ident[:])
+                v_ps.append(v_b)
+            nc.scalar.activation(out=v_out[:, 0, :, :], in_=v_ps[0][:], func=ACT.Copy, scale=inv2[:, 0:1])
+            nc.vector.tensor_scalar(
+                out=v_out[:, 1, :, :], in0=v_ps[1][:], scalar1=inv2[:, 1:2], scalar2=None, op0=ALU.mult
+            )
+            for b in range(B):
+                nc.sync.dma_start(out=out[b].rearrange("(t p k) -> p t k", p=P, k=K), in_=v_out[:, b, :, :])

@@ -18,17 +18,19 @@ PACK = 4
 ROWS = P * PACK
 GROUPS = B * N // ROWS
 GROUPS_PER_BATCH = N // ROWS
+PAIRS = GROUPS // 2
+PAIRS_PER_BATCH = GROUPS_PER_BATCH // 2
 ROUNDS = GROUPS // 2
 BN_EPS = 1e-5
 NORM_EPS = 1e-12
-SCALAR_COLS = 256
+GPSIMD_COLS = 64
 SUM_COLS = 32
 SCORE_LAG = 2
 FIRST_PIECES = 2
 C2_ROUND = 2
-EARLY_CODES = 2
 PLANES = 4
-EARLY = 3
+E_SUMS = 3
+EARLY = 4
 
 FLOPS = 2 * 2 * B * N * D * K
 
@@ -41,7 +43,7 @@ def tile_modelnew_k_kernel(tc, x, clusters, clusters2, bn_gamma, bn_beta, out):
         whole.enter_context(tc.manual_schedule())
         keep = whole.enter_context(tc.tile_pool(name="keep", bufs=1))
         x_pool = whole.enter_context(tc.tile_pool(name="x_pool", bufs=5))
-        grouped_pool = whole.enter_context(tc.tile_pool(name="grouped_pool", bufs=5))
+        grouped_pool = whole.enter_context(tc.tile_pool(name="grouped_pool", bufs=3))
 
         ident = keep.tile([P, P], F32)
         make_identity(nc, ident[:])
@@ -120,11 +122,10 @@ def tile_modelnew_k_kernel(tc, x, clusters, clusters2, bn_gamma, bn_beta, out):
                 nc.tensor.transpose(out=gb_ps[:], in_=gb_f32[:], identity=ident[:])
                 nc.vector.tensor_copy(out=gamma_beta[:], in_=gb_ps[:, 0:2])
 
-            def transpose_group(g):
+            def transpose_group(g, grouped):
                 x_sb = load_group(g, pieces=FIRST_PIECES if g == 0 else 1)
                 x_words = x_sb[:].bitcast(F32)
-                grouped = grouped_pool.tile([P, PACK * ROWS], BF16, align_bytes=64)
-                grouped_words = grouped[:].bitcast(F32).rearrange("q (c u) -> q c u", u=2)
+                grouped_words = grouped.bitcast(F32).rearrange("q (c u) -> q c u", u=2)
                 for half in range(2):
                     xT = xT_ps.tile([P, 2, 2 * P], F32)
                     for jj in range(2):
@@ -140,15 +141,15 @@ def tile_modelnew_k_kernel(tc, x, clusters, clusters2, bn_gamma, bn_beta, out):
                         out=grouped_words[:, 2 * P * half : 2 * P * (half + 1), :],
                         in_=xT[:].rearrange("q u c -> q c u"),
                     )
-                return grouped
 
             for r in range(ROUNDS + SCORE_LAG):
                 this_round = [2 * r, 2 * r + 1] if r < ROUNDS else []
                 s = r - SCORE_LAG
                 last_round = [2 * s, 2 * s + 1] if s >= 0 else []
-                grouped_of = {}
+                if this_round:
+                    grouped = grouped_pool.tile([P, 2, PACK * ROWS], BF16, align_bytes=64)
                 for g in this_round:
-                    grouped_of[g] = transpose_group(g)
+                    transpose_group(g, grouped[:, g % 2, :])
                 for g in last_round:
                     aT = cluster_scores(aT_ps1, g)
                     nc.vector.bn_stats(out=stats[:, g, :], in_=aT[:])
@@ -156,7 +157,7 @@ def tile_modelnew_k_kernel(tc, x, clusters, clusters2, bn_gamma, bn_beta, out):
                     nc.vector.quantize_mx(
                         out=xd_codes[:, g, :].bitcast(FP8X4),
                         scales=scale_plane(g),
-                        in_=grouped_of[g][:],
+                        in_=grouped[:, g % 2, :],
                     )
                 if r == 0:
                     transpose_gamma_beta()
@@ -164,35 +165,52 @@ def tile_modelnew_k_kernel(tc, x, clusters, clusters2, bn_gamma, bn_beta, out):
                     nc.sync.dma_start(out=c2_rows[:], in_=clusters2.rearrange("o (t p) k -> p (o t) k", p=P))
 
         x_of, grouped_of = {}, {}
-        split = D - SCALAR_COLS
+        on_gpsimd = D - GPSIMD_COLS
 
         def regroup(copy, g, first, last):
             x_rows = x_of[g][:].rearrange("p (j d) -> p j d", j=PACK)
-            grouped_cols = grouped_of[g][:].rearrange("p (d j) -> p d j", j=PACK)
+            grouped_cols = grouped_of[g // 2][:, g % 2, :].rearrange("p (d j) -> p d j", j=PACK)
             copy(
                 out=grouped_cols[:, first:last, :].rearrange("p (c i) j -> p c j i", i=4),
                 in_=x_rows[:, :, first:last].rearrange("p j (c i) -> p c j i", i=4),
             )
 
-        def regroup_on_scalar(g, first=split):
-            x_of[g] = load_group(g)
-            grouped_of[g] = grouped_pool.tile([P, PACK * ROWS], BF16, align_bytes=64, name="grouped")
-            regroup(nc.scalar.copy, g, first, D)
+        def start_pair(pair):
+            for g in (2 * pair, 2 * pair + 1):
+                x_of[g] = load_group(g)
+            grouped_of[pair] = grouped_pool.tile([P, 2, PACK * ROWS], BF16, align_bytes=64, name="grouped")
+
+        def regroup_on_scalar(g, last):
+            regroup(nc.scalar.copy, g, 0, last)
 
         def regroup_on_vector(g):
-            regroup(nc.vector.tensor_copy, g, 0, split)
+            regroup(nc.vector.tensor_copy, g, 0, on_gpsimd)
 
-        codes_pool = whole.enter_context(tc.tile_pool(name="codes_pool", bufs=3))
+        def regroup_on_gpsimd(g, one):
+            def copy(out, in_):
+                nc.gpsimd.tensor_scalar(
+                    out=out, in0=in_, scalar1=one, scalar2=0.0, op0=ALU.mult, op1=ALU.add
+                )
+
+            regroup(copy, g, on_gpsimd, D)
+
+        codes_pool = whole.enter_context(tc.tile_pool(name="codes_pool", bufs=2))
         xn_of = {}
 
-        def quantise_rows(g):
-            xn_codes = codes_pool.tile([P, D], U32, align_bytes=64)
-            xn_scales = codes_pool.tile([P, D], U8, align_bytes=64)
-            nc.vector.quantize_mx(out=xn_codes[:].bitcast(FP8X4), scales=xn_scales[:], in_=grouped_of[g][:])
-            xn_of[g] = (xn_codes, xn_scales)
+        def quantise_rows(pair):
+            xn_codes = codes_pool.tile([P, 2 * D], U32, align_bytes=64)
+            xn_scales = codes_pool.tile([P, 2 * D], U8, align_bytes=64)
+            nc.vector.quantize_mx(
+                out=xn_codes[:].bitcast(FP8X4),
+                scales=xn_scales[:],
+                in_=grouped_of[pair][:].rearrange("p g c -> p (g c)"),
+            )
+            xn_of[pair] = (xn_codes, xn_scales)
 
         for g in range(EARLY):
-            regroup_on_scalar(g, first=0)
+            if g % 2 == 0:
+                start_pair(g // 2)
+            regroup_on_scalar(g, D)
         mean_var = keep.tile([P, 2], F32)
         nc.vector.bn_aggr(out=mean_var[:], in_=stats[:].rearrange("k g s -> k (g s)"))
         var_eps = keep.tile([P, 1], F32)
@@ -214,10 +232,11 @@ def tile_modelnew_k_kernel(tc, x, clusters, clusters2, bn_gamma, bn_beta, out):
             op0=ALU.mult,
             op1=ALU.add,
         )
-        for g in range(1, EARLY_CODES):
-            quantise_rows(g)
 
         with ExitStack() as pass2:
+            tail = pass2.enter_context(tc.tile_pool(name="tail", bufs=1))
+            work = pass2.enter_context(tc.tile_pool(name="work", bufs=3))
+            pairs = pass2.enter_context(tc.tile_pool(name="pairs", bufs=2))
             acc_ps = pass2.enter_context(tc.psum_pool(name="acc_ps", bufs=1))
             aT_ps2 = pass2.enter_context(tc.psum_pool(name="aT_ps2", bufs=2))
             z_ps = pass2.enter_context(tc.psum_pool(name="z_ps", bufs=3))
@@ -242,81 +261,95 @@ def tile_modelnew_k_kernel(tc, x, clusters, clusters2, bn_gamma, bn_beta, out):
                     nc.tensor.transpose(out=z[:, j, :], in_=zT_of[g][:, P * j : P * (j + 1)], identity=ident[:])
                 z_of[g] = z
 
-            def exponentials(work, g):
-                z = z_of[g]
-                neg_max = work.tile([P, PACK], F32)
-                nc.vector.tensor_reduce(out=neg_max[:], in_=z[:], axis=AX.X, op=ALU.max, negate=True)
-                e = work.tile([P, PACK, K], F32)
-                e_sum = work.tile([P, PACK], F32)
-                for j in range(PACK):
-                    nc.scalar.activation(
-                        out=e[:, j, :],
-                        in_=z[:, j, :],
-                        func=ACT.Exp,
-                        bias=neg_max[:, j : j + 1],
-                        scale=1.0,
-                        accum_out=e_sum[:, j : j + 1],
-                    )
-                e_of[g] = (e, e_sum)
+            e_sums = []
+            for s in range(E_SUMS):
+                e_sum = tail.tile([P, 2 * PACK + 1], F32, name="e_sum%d" % s)
+                nc.vector.memset(e_sum[:, 2 * PACK : 2 * PACK + 1], 1.0)
+                e_sums.append(e_sum)
 
-            def inverse_sums(work, g):
-                e, e_sum = e_of[g]
-                inv_sum = work.tile([P, PACK], F32)
-                nc.vector.reciprocal(out=inv_sum[:], in_=e_sum[:])
-                inv_sum_of[g] = inv_sum
-                b = g // GROUPS_PER_BATCH
+            neg_max_of = {}
+
+            def maxima(work, g):
+                neg_max = work.tile([P, PACK], F32)
+                nc.vector.tensor_reduce(out=neg_max[:], in_=z_of[g][:], axis=AX.X, op=ALU.max, negate=True)
+                neg_max_of[g] = neg_max
+
+            def exponentials(g):
+                if g % 2 == 0:
+                    e_of[g // 2] = pairs.tile([P, 2, PACK, K], F32, name="e")
                 for j in range(PACK):
+                    s = PACK * (g % 2) + j
+                    nc.scalar.activation(
+                        out=e_of[g // 2][:, g % 2, j, :],
+                        in_=z_of[g][:, j, :],
+                        func=ACT.Exp,
+                        bias=neg_max_of[g][:, j : j + 1],
+                        scale=1.0,
+                        accum_out=e_sums[g // 2 % E_SUMS][:, s : s + 1],
+                    )
+
+            def inverse_sums(pair):
+                inv_sum = pairs.tile([P, 2 * PACK + 1], F32)
+                nc.vector.reciprocal(out=inv_sum[:], in_=e_sums[pair % E_SUMS][:])
+                inv_sum_of[pair] = inv_sum
+
+            def sum_probabilities(pair):
+                b = pair // PAIRS_PER_BATCH
+                for s in range(2 * PACK):
                     nc.tensor.matmul(
                         out=p_sum[:, b, :],
-                        lhsT=e[:, j, :],
-                        rhs=inv_sum[:, j : j + 1].to_broadcast([P, SUM_COLS]),
-                        start=g % GROUPS_PER_BATCH == 0 and j == 0,
-                        stop=g % GROUPS_PER_BATCH == GROUPS_PER_BATCH - 1 and j == PACK - 1,
+                        lhsT=e_of[pair][:, s // PACK, s % PACK, :],
+                        rhs=inv_sum_of[pair][:, s : s + 1].to_broadcast([P, SUM_COLS]),
+                        start=pair % PAIRS_PER_BATCH == 0 and s == 0,
+                        stop=pair % PAIRS_PER_BATCH == PAIRS_PER_BATCH - 1 and s == 2 * PACK - 1,
                     )
 
-            def probabilities(work, g):
-                e, e_sum = e_of[g]
-                p_grouped = work.tile([P, K, PACK], BF16, align_bytes=64)
+            def probabilities(pair):
+                p_grouped = pairs.tile([P, 2, K, PACK], BF16, align_bytes=64)
                 nc.vector.tensor_tensor(
                     out=p_grouped[:],
-                    in0=e[:].rearrange("p j k -> p k j"),
-                    in1=inv_sum_of[g][:].unsqueeze(1).to_broadcast([P, K, PACK]),
+                    in0=e_of[pair][:].rearrange("p g j k -> p g k j"),
+                    in1=inv_sum_of[pair][:, 0 : 2 * PACK]
+                    .rearrange("p (g j) -> p g j", j=PACK)
+                    .unsqueeze(2)
+                    .to_broadcast([P, 2, K, PACK]),
                     op=ALU.mult,
                 )
-                p_grouped_of[g] = p_grouped
+                p_grouped_of[pair] = p_grouped
 
-            def quantise_probabilities(work, g):
-                p_codes = work.tile([P, K], U32, align_bytes=64)
-                p_scales = work.tile([P, K], U8, align_bytes=64)
+            def quantise_probabilities(pair):
+                p_codes = pairs.tile([P, 2 * K], U32, align_bytes=64)
+                p_scales = pairs.tile([P, 2 * K], U8, align_bytes=64)
                 nc.vector.quantize_mx(
                     out=p_codes[:].bitcast(FP8X4),
                     scales=p_scales[:],
-                    in_=p_grouped_of[g][:].rearrange("p k j -> p (k j)"),
+                    in_=p_grouped_of[pair][:].rearrange("p g k j -> p (g k j)"),
                 )
-                p_codes_of[g] = (p_codes, p_scales)
+                p_codes_of[pair] = (p_codes, p_scales)
 
-            def add_to_vlad(g):
-                p_codes, p_scales = p_codes_of[g]
-                xn_codes, xn_scales = xn_of[g]
-                nc.tensor.matmul_mx(
-                    out=vladT[g // GROUPS_PER_BATCH][:],
-                    lhsT=p_codes[:].bitcast(FP8X4),
-                    lhsT_scale=p_scales[:],
-                    rhs=xn_codes[:].bitcast(FP8X4),
-                    rhs_scale=xn_scales[:],
-                    start=g % GROUPS_PER_BATCH == 0,
-                    stop=g % GROUPS_PER_BATCH == GROUPS_PER_BATCH - 1,
-                )
+            def add_to_vlad(pair):
+                p_codes, p_scales = p_codes_of[pair]
+                xn_codes, xn_scales = xn_of[pair]
+                for h in range(2):
+                    nc.tensor.matmul_mx(
+                        out=vladT[pair // PAIRS_PER_BATCH][:],
+                        lhsT=p_codes[:, K * h : K * (h + 1)].bitcast(FP8X4),
+                        lhsT_scale=p_scales[:, K * h : K * (h + 1)],
+                        rhs=xn_codes[:, D * h : D * (h + 1)].bitcast(FP8X4),
+                        rhs_scale=xn_scales[:, D * h : D * (h + 1)],
+                        start=pair % PAIRS_PER_BATCH == 0 and h == 0,
+                        stop=pair % PAIRS_PER_BATCH == PAIRS_PER_BATCH - 1 and h == 1,
+                    )
 
-            def exists(g, first=0):
-                return first <= g < GROUPS
+            def transpose_clusters2():
+                c2_ps = z_ps.tile([P, PACK, P], F32, tag="z")
+                for t in range(PACK):
+                    nc.tensor.transpose(out=c2_ps[:, t, :], in_=c2_f32[:, t, :], identity=ident[:])
+                nc.vector.tensor_copy(out=c2T[:], in_=c2_ps[:].rearrange("k t p -> k (t p)"))
 
-            c2_ps = z_ps.tile([P, PACK, P], F32, tag="z")
-            for t in range(PACK):
-                nc.tensor.transpose(out=c2_ps[:, t, :], in_=c2_f32[:, t, :], identity=ident[:])
-            nc.vector.tensor_copy(out=c2T[:], in_=c2_ps[:].rearrange("k t p -> k (t p)"))
+            def exists(pair):
+                return 0 <= pair < PAIRS
 
-            tail = pass2.enter_context(tc.tile_pool(name="tail", bufs=1))
             neg_p_sum = tail.tile([P, B], F32)
             v = tail.tile([P, B, D], F32)
             squares = tail.tile([P, B, D], F32)
@@ -340,35 +373,47 @@ def tile_modelnew_k_kernel(tc, x, clusters, clusters2, bn_gamma, bn_beta, out):
                     out=squares[:, b, :], in_=v[:, b, :], func=ACT.Square, accum_out=sum_sq[:, b : b + 1]
                 )
 
-            with tc.tile_pool(name="work", bufs=3) as work:
-                for i in range(-3, GROUPS + 1):
-                    if exists(i + 2, first=EARLY):
-                        regroup_on_scalar(i + 2)
-                    if exists(i - 1):
-                        add_to_vlad(i - 1)
-                    if i == GROUPS_PER_BATCH + 1:
-                        negate_p_sum(0)
-                    if i == GROUPS:
-                        finish_vlad(0)
-                        negate_p_sum(1)
-                    if exists(i + 3):
-                        scores(i + 3)
+            for i in range(-2, PAIRS + 1):
+                a, b = 2 * (i + 2), 2 * (i + 2) + 1
+                if exists(i + 2) and a >= EARLY:
+                    start_pair(i + 2)
+                    regroup_on_scalar(b, on_gpsimd)
+                if exists(i + 2):
+                    scores(a)
+                    scores(b)
+                if i == -2:
+                    transpose_clusters2()
+                if i == PAIRS_PER_BATCH + 1:
+                    negate_p_sum(0)
+                if exists(i):
+                    inverse_sums(i)
                     if exists(i + 2):
-                        transpose_scores(i + 2)
-                    if exists(i + 1):
-                        exponentials(work, i + 1)
-                    if exists(i):
-                        inverse_sums(work, i)
-                    if exists(i + 1, first=EARLY_CODES):
-                        quantise_rows(i + 1)
-                    if exists(i):
-                        probabilities(work, i)
-                    if exists(i + 3):
-                        normalise_scores(work, i + 3)
-                    if exists(i + 2, first=EARLY):
-                        regroup_on_vector(i + 2)
-                    if exists(i):
-                        quantise_probabilities(work, i)
+                        for g in (a, b):
+                            regroup_on_gpsimd(g, inv_sum_of[i][:, 2 * PACK : 2 * PACK + 1])
+                if exists(i - 1):
+                    quantise_probabilities(i - 1)
+                    add_to_vlad(i - 1)
+                if i == PAIRS:
+                    finish_vlad(0)
+                    negate_p_sum(1)
+                if exists(i + 1):
+                    for g in (2 * i + 2, 2 * i + 3):
+                        maxima(work, g)
+                    for g in (2 * i + 2, 2 * i + 3):
+                        exponentials(g)
+                if exists(i):
+                    sum_probabilities(i)
+                if exists(i + 2):
+                    for g in (a, b):
+                        normalise_scores(work, g)
+                    for g in (a, b):
+                        transpose_scores(g)
+                if exists(i + 1) and i >= 0:
+                    quantise_rows(i + 1)
+                if exists(i):
+                    probabilities(i)
+                if exists(i + 2) and a >= EARLY:
+                    regroup_on_vector(a)
 
             finish_vlad(1)
             floor1 = tail.tile([P, B], F32)

@@ -24,7 +24,7 @@ ROUNDS = GROUPS // 2
 BN_EPS = 1e-5
 NORM_EPS = 1e-12
 GPSIMD_COLS = 64
-SUM_COLS = 32
+SUM_COLS = 64
 SCORE_LAG = 2
 FIRST_PIECES = 2
 C2_ROUND = 2

@@ -24,12 +24,13 @@ ROUNDS = GROUPS // 2
 BN_EPS = 1e-5
 NORM_EPS = 1e-12
 GPSIMD_COLS = 64
-SUM_COLS = 64
+SUM_COLS = 32
 SCORE_LAG = 2
 FIRST_PIECES = 2
 C2_ROUND = 2
 PLANES = 4
 E_SUMS = 3
+EARLY_ROWS = 2
 EARLY = 4
 
 FLOPS = 2 * 2 * B * N * D * K
@@ -194,7 +195,7 @@ def tile_modelnew_k_kernel(tc, x, clusters, clusters2, bn_gamma, bn_beta, out):
 
             regroup(copy, g, on_gpsimd, D)
 
-        codes_pool = whole.enter_context(tc.tile_pool(name="codes_pool", bufs=2))
+        codes_pool = whole.enter_context(tc.tile_pool(name="codes_pool", bufs=3))
         xn_of = {}
 
         def quantise_rows(pair):
@@ -219,7 +220,6 @@ def tile_modelnew_k_kernel(tc, x, clusters, clusters2, bn_gamma, bn_beta, out):
         nc.gpsimd.tensor_tensor(out=inv_std[:], in0=var_eps[:], in1=minus_half[:, 0:1], op=ALU.pow)
         neg_mean = keep.tile([P, 1], F32)
         nc.vector.tensor_scalar(out=neg_mean[:], in0=mean_var[:, 0:1], scalar1=-1.0, scalar2=None, op0=ALU.mult)
-        quantise_rows(0)
         nc.vector.tensor_copy(out=c2_f32[:], in_=c2_rows[:])
         bn_scale = keep.tile([P, 1], F32)
         nc.vector.tensor_tensor(out=bn_scale[:], in0=inv_std[:], in1=gamma_beta[:, 0:1], op=ALU.mult)
@@ -232,10 +232,12 @@ def tile_modelnew_k_kernel(tc, x, clusters, clusters2, bn_gamma, bn_beta, out):
             op0=ALU.mult,
             op1=ALU.add,
         )
+        quantise_rows(0)
 
         with ExitStack() as pass2:
             tail = pass2.enter_context(tc.tile_pool(name="tail", bufs=1))
-            work = pass2.enter_context(tc.tile_pool(name="work", bufs=3))
+            work = pass2.enter_context(tc.tile_pool(name="work", bufs=2))
+            small = pass2.enter_context(tc.tile_pool(name="small", bufs=4))
             pairs = pass2.enter_context(tc.tile_pool(name="pairs", bufs=2))
             acc_ps = pass2.enter_context(tc.psum_pool(name="acc_ps", bufs=1))
             aT_ps2 = pass2.enter_context(tc.psum_pool(name="aT_ps2", bufs=2))
@@ -269,8 +271,8 @@ def tile_modelnew_k_kernel(tc, x, clusters, clusters2, bn_gamma, bn_beta, out):
 
             neg_max_of = {}
 
-            def maxima(work, g):
-                neg_max = work.tile([P, PACK], F32)
+            def maxima(g):
+                neg_max = small.tile([P, PACK], F32)
                 nc.vector.tensor_reduce(out=neg_max[:], in_=z_of[g][:], axis=AX.X, op=ALU.max, negate=True)
                 neg_max_of[g] = neg_max
 
@@ -293,9 +295,9 @@ def tile_modelnew_k_kernel(tc, x, clusters, clusters2, bn_gamma, bn_beta, out):
                 nc.vector.reciprocal(out=inv_sum[:], in_=e_sums[pair % E_SUMS][:])
                 inv_sum_of[pair] = inv_sum
 
-            def sum_probabilities(pair):
+            def sum_probabilities(pair, h):
                 b = pair // PAIRS_PER_BATCH
-                for s in range(2 * PACK):
+                for s in range(PACK * h, PACK * (h + 1)):
                     nc.tensor.matmul(
                         out=p_sum[:, b, :],
                         lhsT=e_of[pair][:, s // PACK, s % PACK, :],
@@ -352,7 +354,7 @@ def tile_modelnew_k_kernel(tc, x, clusters, clusters2, bn_gamma, bn_beta, out):
 
             neg_p_sum = tail.tile([P, B], F32)
             v = tail.tile([P, B, D], F32)
-            squares = tail.tile([P, B, D], F32)
+            v_out = tail.tile([P, B, PACK, K], F32)
             sum_sq = tail.tile([P, B], F32)
 
             def negate_p_sum(b):
@@ -370,7 +372,7 @@ def tile_modelnew_k_kernel(tc, x, clusters, clusters2, bn_gamma, bn_beta, out):
                     op1=ALU.add,
                 )
                 nc.scalar.activation(
-                    out=squares[:, b, :], in_=v[:, b, :], func=ACT.Square, accum_out=sum_sq[:, b : b + 1]
+                    out=v_out[:, b, :, :].rearrange("p t k -> p (t k)"), in_=v[:, b, :], func=ACT.Square, accum_out=sum_sq[:, b : b + 1]
                 )
 
             for i in range(-2, PAIRS + 1):
@@ -378,6 +380,7 @@ def tile_modelnew_k_kernel(tc, x, clusters, clusters2, bn_gamma, bn_beta, out):
                 if exists(i + 2) and a >= EARLY:
                     start_pair(i + 2)
                     regroup_on_scalar(b, on_gpsimd)
+                    regroup_on_vector(a)
                 if exists(i + 2):
                     scores(a)
                     scores(b)
@@ -390,30 +393,32 @@ def tile_modelnew_k_kernel(tc, x, clusters, clusters2, bn_gamma, bn_beta, out):
                     if exists(i + 2):
                         for g in (a, b):
                             regroup_on_gpsimd(g, inv_sum_of[i][:, 2 * PACK : 2 * PACK + 1])
+                if exists(i):
+                    sum_probabilities(i, 0)
                 if exists(i - 1):
                     quantise_probabilities(i - 1)
                     add_to_vlad(i - 1)
+                if exists(i):
+                    sum_probabilities(i, 1)
                 if i == PAIRS:
                     finish_vlad(0)
                     negate_p_sum(1)
                 if exists(i + 1):
                     for g in (2 * i + 2, 2 * i + 3):
-                        maxima(work, g)
+                        maxima(g)
                     for g in (2 * i + 2, 2 * i + 3):
                         exponentials(g)
-                if exists(i):
-                    sum_probabilities(i)
                 if exists(i + 2):
                     for g in (a, b):
                         normalise_scores(work, g)
                     for g in (a, b):
                         transpose_scores(g)
-                if exists(i + 1) and i >= 0:
+                if exists(i + 1) and i >= EARLY_ROWS - 1:
                     quantise_rows(i + 1)
+                elif i == -1:
+                    quantise_rows(1)
                 if exists(i):
                     probabilities(i)
-                if exists(i + 2) and a >= EARLY:
-                    regroup_on_vector(a)
 
             finish_vlad(1)
             floor1 = tail.tile([P, B], F32)
@@ -436,7 +441,6 @@ def tile_modelnew_k_kernel(tc, x, clusters, clusters2, bn_gamma, bn_beta, out):
             nc.gpsimd.tensor_tensor(out=inv2[:], in0=floor2[:], in1=minus_half[:], op=ALU.pow)
 
             v_unit = tail.tile([P, B, D], F32)
-            v_out = tail.tile([P, B, PACK, K], F32)
             v_ps = []
             for b in range(B):
                 nc.vector.tensor_scalar(

from contextlib import ExitStack

import concourse.mybir as mybir
from concourse.masks import make_identity

F32 = mybir.dt.float32
BF16 = mybir.dt.bfloat16
U32 = mybir.dt.uint32
U8 = mybir.dt.uint8
FP8X4 = mybir.dt.float8_e4m3fn_x4
ACT = mybir.ActivationFunctionType
ALU = mybir.AluOpType
AX = mybir.AxisListType

B, N, D, K = 2, 16384, 512, 128
P = 128
PACK = 4
ROWS = P * PACK
GROUPS = B * N // ROWS
GROUPS_PER_BATCH = N // ROWS
PAIRS = GROUPS // 2
PAIRS_PER_BATCH = GROUPS_PER_BATCH // 2
ROUNDS = GROUPS // 2
BN_EPS = 1e-5
NORM_EPS = 1e-12
GPSIMD_COLS = 64
SUM_COLS = 32
SCORE_LAG = 2
FIRST_PIECES = 2
C2_ROUND = 2
PLANES = 4
E_SUMS = 3
EARLY_ROWS = 2
EARLY = 4

FLOPS = 2 * 2 * B * N * D * K


def tile_modelnew_k_kernel(tc, x, clusters, clusters2, bn_gamma, bn_beta, out):
    nc = tc.nc
    x_groups = x.rearrange("b (g p j) d -> (b g) p (j d)", p=P, j=PACK)

    with ExitStack() as whole:
        whole.enter_context(tc.manual_schedule())
        keep = whole.enter_context(tc.tile_pool(name="keep", bufs=1))
        x_pool = whole.enter_context(tc.tile_pool(name="x_pool", bufs=5))
        grouped_pool = whole.enter_context(tc.tile_pool(name="grouped_pool", bufs=3))

        ident = keep.tile([P, P], F32)
        make_identity(nc, ident[:])
        ones = keep.tile([P, P], F32)
        nc.vector.memset(ones[:], 1.0)
        minus_half = keep.tile([P, B], F32)
        nc.vector.memset(minus_half[:], -0.5)
        zero = keep.tile([P, 1], F32)
        nc.vector.memset(zero[:], 0.0)
        one = keep.tile([P, 1], F32)
        nc.scalar.activation(out=one[:], in_=zero[:], func=ACT.Exp)

        cl_codes = keep.tile([P, K], U32, align_bytes=64)
        cl_scales = keep.tile([P, K], U8, align_bytes=64)
        xd_codes = keep.tile([P, GROUPS, ROWS], U32, align_bytes=64)
        xd_scales = keep.tile([P, GROUPS // PLANES, ROWS], U8, align_bytes=64)
        c2_rows = keep.tile([P, PACK, K], BF16)
        c2_f32 = keep.tile([P, PACK, K], F32)
        c2T = keep.tile([P, D], F32)
        gamma_beta = keep.tile([P, 2], F32)
        stats = keep.tile([P, GROUPS, 6], F32)

        def load_group(g, pieces=1):
            x_sb = x_pool.tile([P, PACK * D], BF16)
            width = PACK * D // pieces
            for i in range(pieces):
                cols = slice(i * width, (i + 1) * width)
                nc.sync.dma_start(out=x_sb[:, cols], in_=x_groups[g][:, cols])
            return x_sb

        def scale_plane(g):
            first = 4 * (g // (GROUPS // PLANES))
            return xd_scales[first:P, g % (GROUPS // PLANES), :]

        def cluster_scores(psum_pool, g):
            aT = psum_pool.tile([P, ROWS], F32)
            nc.tensor.matmul_mx(
                out=aT[:],
                lhsT=cl_codes[:].bitcast(FP8X4),
                lhsT_scale=cl_scales[:],
                rhs=xd_codes[:, g, :].bitcast(FP8X4),
                rhs_scale=scale_plane(g),
                start=True,
                stop=True,
            )
            return aT

        with ExitStack() as pass1:
            setup = pass1.enter_context(tc.tile_pool(name="setup", bufs=1))
            xT_ps = pass1.enter_context(tc.psum_pool(name="xT_ps", bufs=6))
            aT_ps1 = pass1.enter_context(tc.psum_pool(name="aT_ps1", bufs=2))

            cl_rows = setup.tile([P, PACK, K], BF16)
            for u in range(2):
                nc.scalar.dma_start(
                    out=cl_rows[:, 2 * u : 2 * u + 2, :],
                    in_=clusters[256 * u : 256 * (u + 1), :].rearrange("(q e) k -> q e k", e=2),
                )
            gb_rows = setup.tile([P, P], BF16)
            nc.vector.memset(gb_rows[:], 0.0)
            nc.scalar.dma_start(out=gb_rows[0:1, :], in_=bn_gamma.rearrange("(o k) -> o k", o=1))
            nc.scalar.dma_start(out=gb_rows[1:2, :], in_=bn_beta.rearrange("(o k) -> o k", o=1))

            cl_grouped = setup.tile([P, K, PACK], BF16, align_bytes=64)
            nc.vector.tensor_copy(out=cl_grouped[:], in_=cl_rows[:].rearrange("q t k -> q k t"))
            nc.vector.quantize_mx(
                out=cl_codes[:].bitcast(FP8X4),
                scales=cl_scales[:],
                in_=cl_grouped[:].rearrange("q k t -> q (k t)"),
            )
            gb_f32 = setup.tile([P, P], F32)
            nc.vector.tensor_copy(out=gb_f32[:], in_=gb_rows[:])

            def transpose_gamma_beta():
                gb_ps = xT_ps.tile([P, P], F32, tag="xT")
                nc.tensor.transpose(out=gb_ps[:], in_=gb_f32[:], identity=ident[:])
                nc.vector.tensor_copy(out=gamma_beta[:], in_=gb_ps[:, 0:2])

            def transpose_group(g, grouped):
                x_sb = load_group(g, pieces=FIRST_PIECES if g == 0 else 1)
                x_words = x_sb[:].bitcast(F32)
                grouped_words = grouped.bitcast(F32).rearrange("q (c u) -> q c u", u=2)
                for half in range(2):
                    xT = xT_ps.tile([P, 2, 2 * P], F32)
                    for jj in range(2):
                        j = 2 * half + jj
                        for u in range(2):
                            first = 256 * j + 128 * u
                            nc.tensor.transpose(
                                out=xT[:, u, P * jj : P * (jj + 1)],
                                in_=x_words[:, first : first + P],
                                identity=ident[:],
                            )
                    nc.scalar.copy(
                        out=grouped_words[:, 2 * P * half : 2 * P * (half + 1), :],
                        in_=xT[:].rearrange("q u c -> q c u"),
                    )

            for r in range(ROUNDS + SCORE_LAG):
                this_round = [2 * r, 2 * r + 1] if r < ROUNDS else []
                s = r - SCORE_LAG
                last_round = [2 * s, 2 * s + 1] if s >= 0 else []
                if this_round:
                    grouped = grouped_pool.tile([P, 2, PACK * ROWS], BF16, align_bytes=64)
                for g in this_round:
                    transpose_group(g, grouped[:, g % 2, :])
                for g in last_round:
                    aT = cluster_scores(aT_ps1, g)
                    nc.vector.bn_stats(out=stats[:, g, :], in_=aT[:])
                for g in this_round:
                    nc.vector.quantize_mx(
                        out=xd_codes[:, g, :].bitcast(FP8X4),
                        scales=scale_plane(g),
                        in_=grouped[:, g % 2, :],
                    )
                if r == 0:
                    transpose_gamma_beta()
                if r == C2_ROUND:
                    nc.sync.dma_start(out=c2_rows[:], in_=clusters2.rearrange("o (t p) k -> p (o t) k", p=P))

        x_of, grouped_of = {}, {}
        on_gpsimd = D - GPSIMD_COLS

        def regroup(copy, g, first, last):
            x_rows = x_of[g][:].rearrange("p (j d) -> p j d", j=PACK)
            grouped_cols = grouped_of[g // 2][:, g % 2, :].rearrange("p (d j) -> p d j", j=PACK)
            copy(
                out=grouped_cols[:, first:last, :].rearrange("p (c i) j -> p c j i", i=4),
                in_=x_rows[:, :, first:last].rearrange("p j (c i) -> p c j i", i=4),
            )

        def start_pair(pair):
            for g in (2 * pair, 2 * pair + 1):
                x_of[g] = load_group(g)
            grouped_of[pair] = grouped_pool.tile([P, 2, PACK * ROWS], BF16, align_bytes=64, name="grouped")

        def regroup_on_scalar(g, last):
            regroup(nc.scalar.copy, g, 0, last)

        def regroup_on_vector(g):
            regroup(nc.vector.tensor_copy, g, 0, on_gpsimd)

        def regroup_on_gpsimd(g, one):
            def copy(out, in_):
                nc.gpsimd.tensor_scalar(
                    out=out, in0=in_, scalar1=one, scalar2=0.0, op0=ALU.mult, op1=ALU.add
                )

            regroup(copy, g, on_gpsimd, D)

        codes_pool = whole.enter_context(tc.tile_pool(name="codes_pool", bufs=3))
        xn_of = {}

        def quantise_rows(pair):
            xn_codes = codes_pool.tile([P, 2 * D], U32, align_bytes=64)
            xn_scales = codes_pool.tile([P, 2 * D], U8, align_bytes=64)
            nc.vector.quantize_mx(
                out=xn_codes[:].bitcast(FP8X4),
                scales=xn_scales[:],
                in_=grouped_of[pair][:].rearrange("p g c -> p (g c)"),
            )
            xn_of[pair] = (xn_codes, xn_scales)

        for g in range(EARLY):
            if g % 2 == 0:
                start_pair(g // 2)
            regroup_on_scalar(g, D)
        mean_var = keep.tile([P, 2], F32)
        nc.vector.bn_aggr(out=mean_var[:], in_=stats[:].rearrange("k g s -> k (g s)"))
        var_eps = keep.tile([P, 1], F32)
        nc.vector.tensor_scalar(out=var_eps[:], in0=mean_var[:, 1:2], scalar1=BN_EPS, scalar2=None, op0=ALU.add)
        inv_std = keep.tile([P, 1], F32)
        nc.gpsimd.tensor_tensor(out=inv_std[:], in0=var_eps[:], in1=minus_half[:, 0:1], op=ALU.pow)
        neg_mean = keep.tile([P, 1], F32)
        nc.vector.tensor_scalar(out=neg_mean[:], in0=mean_var[:, 0:1], scalar1=-1.0, scalar2=None, op0=ALU.mult)
        nc.vector.tensor_copy(out=c2_f32[:], in_=c2_rows[:])
        bn_scale = keep.tile([P, 1], F32)
        nc.vector.tensor_tensor(out=bn_scale[:], in0=inv_std[:], in1=gamma_beta[:, 0:1], op=ALU.mult)
        bn_shift = keep.tile([P, 1], F32)
        nc.vector.scalar_tensor_tensor(
            out=bn_shift[:],
            in0=neg_mean[:],
            scalar=bn_scale[:],
            in1=gamma_beta[:, 1:2],
            op0=ALU.mult,
            op1=ALU.add,
        )
        quantise_rows(0)

        with ExitStack() as pass2:
            tail = pass2.enter_context(tc.tile_pool(name="tail", bufs=1))
            work = pass2.enter_context(tc.tile_pool(name="work", bufs=2))
            small = pass2.enter_context(tc.tile_pool(name="small", bufs=4))
            pairs = pass2.enter_context(tc.tile_pool(name="pairs", bufs=2))
            acc_ps = pass2.enter_context(tc.psum_pool(name="acc_ps", bufs=1))
            aT_ps2 = pass2.enter_context(tc.psum_pool(name="aT_ps2", bufs=2))
            z_ps = pass2.enter_context(tc.psum_pool(name="z_ps", bufs=3))
            vladT = [acc_ps.tile([P, D], F32, name="vladT%d" % b) for b in range(B)]
            p_sum = acc_ps.tile([P, B, SUM_COLS], F32)

            aT_of, zT_of, z_of, e_of, inv_sum_of, p_grouped_of, p_codes_of = {}, {}, {}, {}, {}, {}, {}

            def scores(g):
                aT_of[g] = cluster_scores(aT_ps2, g)

            def normalise_scores(work, g):
                zT = work.tile([P, ROWS], F32)
                nc.scalar.activation(
                    out=zT[:], in_=aT_of[g][:], func=ACT.Identity, bias=bn_shift[:], scale=bn_scale[:]
                )
                zT_of[g] = zT

            def transpose_scores(g):
                z = z_ps.tile([P, PACK, K], F32)
                for j in range(PACK):
                    nc.tensor.transpose(out=z[:, j, :], in_=zT_of[g][:, P * j : P * (j + 1)], identity=ident[:])
                z_of[g] = z

            e_sums = []
            for s in range(E_SUMS):
                e_sum = tail.tile([P, 2 * PACK + 1], F32, name="e_sum%d" % s)
                nc.vector.memset(e_sum[:, 2 * PACK : 2 * PACK + 1], 1.0)
                e_sums.append(e_sum)

            neg_max_of = {}

            def maxima(g):
                neg_max = small.tile([P, PACK], F32)
                nc.vector.tensor_reduce(out=neg_max[:], in_=z_of[g][:], axis=AX.X, op=ALU.max, negate=True)
                neg_max_of[g] = neg_max

            def exponentials(g):
                if g % 2 == 0:
                    e_of[g // 2] = pairs.tile([P, 2, PACK, K], F32, name="e")
                for j in range(PACK):
                    s = PACK * (g % 2) + j
                    nc.scalar.activation(
                        out=e_of[g // 2][:, g % 2, j, :],
                        in_=z_of[g][:, j, :],
                        func=ACT.Exp,
                        bias=neg_max_of[g][:, j : j + 1],
                        scale=1.0,
                        accum_out=e_sums[g // 2 % E_SUMS][:, s : s + 1],
                    )

            def inverse_sums(pair):
                inv_sum = pairs.tile([P, 2 * PACK + 1], F32)
                nc.vector.reciprocal(out=inv_sum[:], in_=e_sums[pair % E_SUMS][:])
                inv_sum_of[pair] = inv_sum

            def sum_probabilities(pair, h):
                b = pair // PAIRS_PER_BATCH
                for s in range(PACK * h, PACK * (h + 1)):
                    nc.tensor.matmul(
                        out=p_sum[:, b, :],
                        lhsT=e_of[pair][:, s // PACK, s % PACK, :],
                        rhs=inv_sum_of[pair][:, s : s + 1].to_broadcast([P, SUM_COLS]),
                        start=pair % PAIRS_PER_BATCH == 0 and s == 0,
                        stop=pair % PAIRS_PER_BATCH == PAIRS_PER_BATCH - 1 and s == 2 * PACK - 1,
                    )

            def probabilities(pair):
                p_grouped = pairs.tile([P, 2, K, PACK], BF16, align_bytes=64)
                nc.vector.tensor_tensor(
                    out=p_grouped[:],
                    in0=e_of[pair][:].rearrange("p g j k -> p g k j"),
                    in1=inv_sum_of[pair][:, 0 : 2 * PACK]
                    .rearrange("p (g j) -> p g j", j=PACK)
                    .unsqueeze(2)
                    .to_broadcast([P, 2, K, PACK]),
                    op=ALU.mult,
                )
                p_grouped_of[pair] = p_grouped

            def quantise_probabilities(pair):
                p_codes = pairs.tile([P, 2 * K], U32, align_bytes=64)
                p_scales = pairs.tile([P, 2 * K], U8, align_bytes=64)
                nc.vector.quantize_mx(
                    out=p_codes[:].bitcast(FP8X4),
                    scales=p_scales[:],
                    in_=p_grouped_of[pair][:].rearrange("p g k j -> p (g k j)"),
                )
                p_codes_of[pair] = (p_codes, p_scales)

            def add_to_vlad(pair):
                p_codes, p_scales = p_codes_of[pair]
                xn_codes, xn_scales = xn_of[pair]
                for h in range(2):
                    nc.tensor.matmul_mx(
                        out=vladT[pair // PAIRS_PER_BATCH][:],
                        lhsT=p_codes[:, K * h : K * (h + 1)].bitcast(FP8X4),
                        lhsT_scale=p_scales[:, K * h : K * (h + 1)],
                        rhs=xn_codes[:, D * h : D * (h + 1)].bitcast(FP8X4),
                        rhs_scale=xn_scales[:, D * h : D * (h + 1)],
                        start=pair % PAIRS_PER_BATCH == 0 and h == 0,
                        stop=pair % PAIRS_PER_BATCH == PAIRS_PER_BATCH - 1 and h == 1,
                    )

            def transpose_clusters2():
                c2_ps = z_ps.tile([P, PACK, P], F32, tag="z")
                for t in range(PACK):
                    nc.tensor.transpose(out=c2_ps[:, t, :], in_=c2_f32[:, t, :], identity=ident[:])
                nc.vector.tensor_copy(out=c2T[:], in_=c2_ps[:].rearrange("k t p -> k (t p)"))

            def exists(pair):
                return 0 <= pair < PAIRS

            neg_p_sum = tail.tile([P, B], F32)
            v = tail.tile([P, B, D], F32)
            v_out = tail.tile([P, B, PACK, K], F32)
            sum_sq = tail.tile([P, B], F32)

            def negate_p_sum(b):
                nc.vector.tensor_scalar(
                    out=neg_p_sum[:, b : b + 1], in0=p_sum[:, b, 0:1], scalar1=-1.0, scalar2=None, op0=ALU.mult
                )

            def finish_vlad(b):
                nc.vector.scalar_tensor_tensor(
                    out=v[:, b, :],
                    in0=c2T[:],
                    scalar=neg_p_sum[:, b : b + 1],
                    in1=vladT[b][:],
                    op0=ALU.mult,
                    op1=ALU.add,
                )
                nc.scalar.activation(
                    out=v_out[:, b, :, :].rearrange("p t k -> p (t k)"), in_=v[:, b, :], func=ACT.Square, accum_out=sum_sq[:, b : b + 1]
                )

            for i in range(-2, PAIRS + 1):
                a, b = 2 * (i + 2), 2 * (i + 2) + 1
                if exists(i + 2) and a >= EARLY:
                    start_pair(i + 2)
                    regroup_on_scalar(b, on_gpsimd)
                    regroup_on_vector(a)
                if exists(i + 2):
                    scores(a)
                    scores(b)
                if i == -2:
                    transpose_clusters2()
                if i == PAIRS_PER_BATCH + 1:
                    negate_p_sum(0)
                if exists(i):
                    inverse_sums(i)
                    if exists(i + 2):
                        for g in (a, b):
                            regroup_on_gpsimd(g, inv_sum_of[i][:, 2 * PACK : 2 * PACK + 1])
                if exists(i):
                    sum_probabilities(i, 0)
                if exists(i - 1):
                    quantise_probabilities(i - 1)
                    add_to_vlad(i - 1)
                if exists(i):
                    sum_probabilities(i, 1)
                if i == PAIRS:
                    finish_vlad(0)
                    negate_p_sum(1)
                if exists(i + 1):
                    for g in (2 * i + 2, 2 * i + 3):
                        maxima(g)
                    for g in (2 * i + 2, 2 * i + 3):
                        exponentials(g)
                if exists(i + 2):
                    for g in (a, b):
                        normalise_scores(work, g)
                    for g in (a, b):
                        transpose_scores(g)
                if exists(i + 1) and i >= EARLY_ROWS - 1:
                    quantise_rows(i + 1)
                elif i == -1:
                    quantise_rows(1)
                if exists(i):
                    probabilities(i)

            finish_vlad(1)
            floor1 = tail.tile([P, B], F32)
            nc.vector.tensor_scalar(
                out=floor1[:], in0=sum_sq[:], scalar1=NORM_EPS * NORM_EPS, scalar2=None, op0=ALU.max
            )
            inv1 = tail.tile([P, B], F32)
            nc.gpsimd.tensor_tensor(out=inv1[:], in0=floor1[:], in1=minus_half[:], op=ALU.pow)
            inv_floor1 = tail.tile([P, B], F32)
            nc.vector.reciprocal(out=inv_floor1[:], in_=floor1[:])
            col_sq = tail.tile([P, B], F32)
            nc.vector.tensor_tensor(out=col_sq[:], in0=sum_sq[:], in1=inv_floor1[:], op=ALU.mult)
            total_ps = aT_ps2.tile([P, B], F32, tag="aT")
            nc.tensor.matmul(out=total_ps[:], lhsT=ones[:], rhs=col_sq[:], start=True, stop=True)
            floor2 = tail.tile([P, B], F32)
            nc.vector.tensor_scalar(
                out=floor2[:], in0=total_ps[:], scalar1=NORM_EPS * NORM_EPS, scalar2=None, op0=ALU.max
            )
            inv2 = tail.tile([P, B], F32)
            nc.gpsimd.tensor_tensor(out=inv2[:], in0=floor2[:], in1=minus_half[:], op=ALU.pow)

            v_unit = tail.tile([P, B, D], F32)
            v_ps = []
            for b in range(B):
                nc.vector.tensor_scalar(
                    out=v_unit[:, b, :], in0=v[:, b, :], scalar1=inv1[:, b : b + 1], scalar2=None, op0=ALU.mult
                )
                v_b = z_ps.tile([P, PACK, K], F32, tag="z")
                for t in range(PACK):
                    nc.tensor.transpose(out=v_b[:, t, :], in_=v_unit[:, b, P * t : P * (t + 1)], identity=ident[:])
                v_ps.append(v_b)
            nc.scalar.activation(out=v_out[:, 0, :, :], in_=v_ps[0][:], func=ACT.Copy, scale=inv2[:, 0:1])
            nc.vector.tensor_scalar(
                out=v_out[:, 1, :, :], in0=v_ps[1][:], scalar1=inv2[:, 1:2], scalar2=None, op0=ALU.mult
            )
            for b in range(B):
                nc.sync.dma_start(out=out[b].rearrange("(t p k) -> p t k", p=P, k=K), in_=v_out[:, b, :, :])
